import numpy as np
import ml_dtypes


def mxq(x, axis, fmt="e4m3"):
    dtype, down = {"e4m3": (ml_dtypes.float8_e4m3fn, 7), "e5m2": (ml_dtypes.float8_e5m2, 14)}[fmt]
    v = np.moveaxis(np.asarray(x, np.float32).astype(ml_dtypes.bfloat16).astype(np.float64), axis, -1)
    blocks = v.reshape(v.shape[:-1] + (-1, 32))
    amax = np.abs(blocks).max(-1, keepdims=True)
    byte = np.maximum(np.where(amax > 0, np.frexp(amax)[1] - 1 + 127, 0) - down, 1)
    scale = np.exp2(byte - 127.0)
    codes = (blocks / scale).astype(np.float32).astype(dtype).astype(np.float64)
    return np.moveaxis((codes * scale).reshape(v.shape), -1, axis)


WIDE = False


def mx_kscale(k):
    if not WIDE:
        return np.ones(k)
    levels = np.array([10, -10, 5, -5, 0])
    a = np.random.permutation(np.resize(levels, k // 512 * 4)).reshape(k // 512, 4)
    idx = np.arange(k)
    return np.exp2(a[idx // 512, idx % 128 // 32])


BF16 = ml_dtypes.bfloat16


def bf(x):
    return np.asarray(x, np.float32).astype(BF16)


def f64(x):
    return np.asarray(x).astype(np.float64)


E2M1 = np.array([0.0, 0.5, 1.0, 1.5, 2.0, 3.0, 4.0, 6.0, -0.0, -0.5, -1.0, -1.5, -2.0, -3.0, -4.0, -6.0])


def pack_weight(w, fmt):
    k, n = w.shape
    w = f64(bf(w)).reshape(k // 32, 32, n)
    amax = np.abs(w).max(1)
    if fmt == "e4m3":
        byte = np.frexp(amax)[1] - 1 + 127 - 7
    else:
        mant, ex = np.frexp(amax / 6.0)
        byte = np.where(mant > 0.5, ex, ex - 1) + 127
    byte = np.clip(np.where(amax > 0, byte, 1), 1, 254)
    scaled = (w * np.exp2(127.0 - byte)[:, None, :]).reshape(k, n).astype(np.float32)
    by_word = np.ascontiguousarray(scaled.reshape(k // 512, 128, 4, n).transpose(0, 1, 3, 2))
    if fmt == "e4m3":
        words = by_word.astype(ml_dtypes.float8_e4m3fn).view(np.uint8)
    else:
        c = by_word.astype(ml_dtypes.float4_e2m1fn).view(np.uint8) & 0xF
        words = c[..., 0::2] | (c[..., 1::2] << 4)
    return np.ascontiguousarray(words), np.ascontiguousarray(byte.astype(np.uint8).reshape(k // 512, 16, n))


def unpack_weight(words, scales, fmt):
    g, p, n, _ = words.shape
    if fmt == "e4m3":
        vals = np.ascontiguousarray(words).view(ml_dtypes.float8_e4m3fn).astype(np.float64)
    else:
        nib = np.empty((g, p, n, 4), np.uint8)
        nib[..., 0::2] = words & 0xF
        nib[..., 1::2] = words >> 4
        vals = E2M1[nib]
    vals = vals * np.repeat(np.exp2(scales.astype(np.float64) - 127.0), 8, axis=1)[..., None]
    return vals.transpose(0, 1, 3, 2).reshape(g * 512, n)


B, S, D, H, KV, DH, QB = 4, 2048, 512, 2, 1, 128, 512
HALF = DH // 2
EPS = 1e-6
FMT = "e4m3"


def rope_tables():
    inv_freq = 1.0 / (10000.0 ** (np.arange(HALF) / HALF))
    ang = np.arange(S)[:, None] * inv_freq[None, :]
    ang = np.concatenate([ang, ang], axis=-1)
    return np.sin(ang), np.cos(ang)


def rmsnorm(u, scale, shift):
    rms = np.sqrt(np.mean(u * u, axis=-1, keepdims=True) + EPS)
    return u / rms * (1.0 + scale) + shift


def apply_rope(u, sin, cos):
    rot = np.concatenate([-u[..., HALF:], u[..., :HALF]], axis=-1)
    return u * cos[None, None, :S, :] + rot * sin[None, None, :S, :]


def heads(u, n):
    return u.reshape(B, S, n, DH).transpose(0, 2, 1, 3)


def setup_inputs():
    s = mx_kscale(D)
    sin, cos = rope_tables()
    x = bf(np.random.standard_normal((B, S, D)) * s)
    wq_words, wq_scales = pack_weight(np.ascontiguousarray((np.random.standard_normal((H * DH, D)) / np.sqrt(D) / s).T), FMT)
    wk_words, wk_scales = pack_weight(np.ascontiguousarray((np.random.standard_normal((KV * DH, D)) / np.sqrt(D) / s).T), FMT)
    wv_words, wv_scales = pack_weight(np.ascontiguousarray((np.random.standard_normal((KV * DH, D)) * 2.0 / np.sqrt(D) / s).T), FMT)
    return {"x": x,
            "sin_thetas": bf(sin), "cos_thetas": bf(cos),
            "wq_words": wq_words, "wq_scales": wq_scales,
            "wk_words": wk_words, "wk_scales": wk_scales,
            "wv_words": wv_words, "wv_scales": wv_scales,
            "q_scale": bf(np.random.standard_normal(DH) * 0.1), "q_shift": bf(np.random.standard_normal(DH) * 0.1),
            "k_scale": bf(np.random.standard_normal(DH) * 0.1), "k_shift": bf(np.random.standard_normal(DH) * 0.1)}


def reference(x, sin_thetas, cos_thetas, wq_words, wq_scales, wk_words, wk_scales, wv_words, wv_scales, q_scale, q_shift, k_scale, k_shift):
    xq = mxq(f64(x), 2, "e4m3")
    q = heads(xq @ unpack_weight(wq_words, wq_scales, FMT), H)
    k = heads(xq @ unpack_weight(wk_words, wk_scales, FMT), KV)
    v = heads(xq @ unpack_weight(wv_words, wv_scales, FMT), KV)
    q = rmsnorm(q, f64(q_scale), f64(q_shift))
    k = rmsnorm(k, f64(k_scale), f64(k_shift))
    q = apply_rope(q, f64(sin_thetas), f64(cos_thetas))
    k = apply_rope(k, f64(sin_thetas), f64(cos_thetas))
    return q, k, v

@@ -1,0 +1,293 @@
+from contextlib import ExitStack
+
+import concourse.mybir as mybir
+from concourse.masks import make_identity
+
+F32 = mybir.dt.float32
+BF16 = mybir.dt.bfloat16
+I32 = mybir.dt.int32
+U8 = mybir.dt.uint8
+U32 = mybir.dt.uint32
+FP8X4 = mybir.dt.float8_e4m3fn_x4
+ALU = mybir.AluOpType
+ACT = mybir.ActivationFunctionType
+
+P = 128
+B = 4
+S = 2048
+D = 512
+H = 2
+DH = 128
+HALF = DH // 2
+EPS = 1e-6
+T = S // P
+N_ALL = (H + 2) * DH
+BLOCKS = B * (H + 1)
+BANK_BLOCKS = 4
+ST = 2
+TABLE_T = 4
+
+FLOPS = 2 * B * S * D * N_ALL
+
+
+def tile_groupqueryattention_pa_t_kernel(
+    tc,
+    x,
+    sin_thetas,
+    cos_thetas,
+    wq_words,
+    wq_scales,
+    wk_words,
+    wk_scales,
+    wv_words,
+    wv_scales,
+    q_scale,
+    q_shift,
+    k_scale,
+    k_shift,
+    out_0,
+    out_1,
+    out_2,
+):
+    nc = tc.nc
+    x_view = x.rearrange("b (p t) k -> p b t k", t=T)
+    q_view = out_0.rearrange("b h (p t) d -> p (b h) t d", t=T)
+    k_view = out_1.rearrange("b h (p t) d -> p (b h) t d", t=T)
+    v_view = out_2.rearrange("b h (p t) d -> p (b h) t d", t=T)
+
+    with ExitStack() as ctx:
+        ctx.enter_context(tc.manual_schedule())
+        const = ctx.enter_context(tc.tile_pool(name="const", bufs=1))
+        xpool = ctx.enter_context(tc.tile_pool(name="xpool", bufs=1))
+        quant = ctx.enter_context(tc.tile_pool(name="quant", bufs=2))
+        work = ctx.enter_context(tc.tile_pool(name="work", bufs=3))
+        stage = ctx.enter_context(tc.tile_pool(name="stage", bufs=2))
+        psum = ctx.enter_context(tc.psum_pool(name="psum", bufs=2))
+
+        x_tiles = []
+        for t in range(T):
+            xt_sb = xpool.tile([P, B, D], BF16, name="x%d" % t)
+            x_tiles.append(xt_sb)
+
+        def load_x(t):
+            nc.sync.dma_start(out=x_tiles[t][:], in_=x_view[:, :, t, :])
+
+        load_x(0)
+        load_x(1)
+        w_codes = const.tile([P, 4 * N_ALL], U8, align_bytes=64)
+        w_scales = const.tile([P, N_ALL], U8, align_bytes=64)
+        nc.vector.memset(w_scales[:].bitcast(I32), 0)
+        col = 0
+        for words, scales in ((wq_words, wq_scales), (wk_words, wk_scales), (wv_words, wv_scales)):
+            n = words.shape[2]
+            nc.sync.dma_start(
+                out=w_codes[:, 4 * col : 4 * (col + n)].bitcast(I32),
+                in_=words[0].rearrange("p n t -> p (n t)").bitcast(I32),
+            )
+            for quad in range(4):
+                nc.sync.dma_start(
+                    out=w_scales[32 * quad : 32 * quad + 4, col : col + n].bitcast(I32),
+                    in_=scales[0, 4 * quad : 4 * quad + 4, :].bitcast(I32),
+                )
+            col += n
+        for t in range(2, T):
+            load_x(t)
+
+        par_b = const.tile([P, 4, DH], BF16)
+        for i, vec in enumerate((q_scale, k_scale, q_shift, k_shift)):
+            nc.scalar.dma_start(out=par_b[:, i, :], in_=vec.partition_broadcast(P))
+        cos_sb = const.tile([P, T, DH], BF16)
+        sin_sb = const.tile([P, T, DH], BF16)
+        nc.scalar.dma_start(out=cos_sb[:], in_=cos_thetas.rearrange("(p t) d -> p t d", t=T))
+        nc.scalar.dma_start(out=sin_sb[:], in_=sin_thetas.rearrange("(p t) d -> p t d", t=T))
+
+        ident_f32 = const.tile([P, P], F32)
+        make_identity(nc, ident_f32[:])
+        ident_bf = const.tile([P, P], BF16)
+        make_identity(nc, ident_bf[:])
+        eps_col = const.tile([P, 1], F32)
+        nc.vector.memset(eps_col[:], EPS)
+        warm = const.tile([P, 1], F32)
+        nc.scalar.activation(out=warm[:], in_=eps_col[:], func=ACT.Sqrt)
+
+        gain = const.tile([P, 2, DH], F32)
+        nc.vector.tensor_scalar_add(out=gain[:], in0=par_b[:, 0:2, :], scalar1=1.0)
+        gain_rot = const.tile([P, 2, DH], F32)
+        nc.vector.tensor_scalar_mul(out=gain_rot[:, :, 0:HALF], in0=gain[:, :, HALF:DH], scalar1=-1.0)
+        nc.vector.tensor_copy(out=gain_rot[:, :, HALF:DH], in_=gain[:, :, 0:HALF])
+
+        a_tab = const.tile([P, T, 2, DH], F32)
+        b_tab = const.tile([P, T, 2, DH], F32)
+
+        def build_tables(engine, t0):
+            for tab, trig, vec in ((a_tab, cos_sb, gain), (b_tab, sin_sb, gain_rot)):
+                engine.tensor_tensor(
+                    out=tab[:, t0 : t0 + TABLE_T, :, :],
+                    in0=trig[:, t0 : t0 + TABLE_T, :].unsqueeze(2).to_broadcast([P, TABLE_T, 2, DH]),
+                    in1=vec[:].unsqueeze(1).to_broadcast([P, TABLE_T, 2, DH]),
+                    op=ALU.mult,
+                )
+
+        def transpose_x(t):
+            grouped = quant.tile([P, B, P, 2], F32, align_bytes=64, name="grouped")
+            for j in range(B // 2):
+                xt = psum.tile([P, 2, 2, P], F32, tag="xt", name="xt")
+                for i in range(2):
+                    x_words = x_tiles[t][:, 2 * j + i, :].bitcast(F32)
+                    for u in range(2):
+                        nc.tensor.transpose(xt[:, i, u, :], x_words[:, u : D // 2 : 2], ident_f32[:])
+                nc.scalar.copy(
+                    out=grouped[:, 2 * j : 2 * j + 2, :, :],
+                    in_=xt[:].rearrange("p i u r -> p i r u"),
+                )
+            return grouped
+
+        def quantise(grouped):
+            codes = quant.tile([P, B * P], U32, align_bytes=64, name="codes")
+            planes = quant.tile([P, B * P], U8, align_bytes=64, name="planes")
+            nc.vector.quantize_mx(
+                out=codes[:].bitcast(FP8X4),
+                scales=planes[:],
+                in_=grouped[:].rearrange("p b r u -> p (b r u)").bitcast(BF16),
+            )
+            return codes, planes
+
+        out_tiles = {}
+
+        def project(t, codes, planes):
+            def pass_mx(out, b, c0, c1):
+                nc.tensor.matmul_mx(
+                    out=out,
+                    lhsT=codes[:, b * P : (b + 1) * P].bitcast(FP8X4),
+                    lhsT_scale=planes[:, b * P : (b + 1) * P],
+                    rhs=w_codes[:, 4 * c0 : 4 * c1].bitcast(FP8X4),
+                    rhs_scale=w_scales[:, c0:c1],
+                    start=True,
+                    stop=True,
+                )
+
+            vbanks = []
+            for j in range(BLOCKS // BANK_BLOCKS):
+                vb = psum.tile([P, BANK_BLOCKS * DH], F32, tag="vbank", bufs=3, name="vb")
+                vbanks.append(vb)
+            for b in range(B):
+                pass_mx(vbanks[b // 2][:, (b % 2) * H * DH : (b % 2 + 1) * H * DH], b, 0, H * DH)
+            for b in range(B):
+                pass_mx(vbanks[2][:, b * DH : (b + 1) * DH], b, H * DH, (H + 1) * DH)
+            if t % ST == 0:
+                out_tiles["v"] = stage.tile([P, B, ST, DH], F32, name="rv")
+            rv = out_tiles["v"]
+            sumsq = work.tile([P, BLOCKS], F32, name="sumsq")
+            for b in range(B):
+                sbank = psum.tile([P, N_ALL], F32, tag="sbank", name="sbank")
+                pass_mx(sbank[:], b, 0, N_ALL)
+                nc.scalar.copy(out=rv[:, b, t % ST, :], in_=sbank[:, (H + 1) * DH : N_ALL])
+                for h in range(H + 1):
+                    blk = H * b + h if h < H else H * B + b
+                    junk = work.tile([P, DH], F32, name="junk")
+                    nc.scalar.activation(
+                        out=junk[:], in_=sbank[:, h * DH : (h + 1) * DH], func=ACT.Square,
+                        accum_out=sumsq[:, blk : blk + 1],
+                    )
+            if t % ST == ST - 1:
+                nc.sync.dma_start(out=v_view[:, :, t - ST + 1 : t + 1, :], in_=rv[:])
+            rms = work.tile([P, BLOCKS], F32, name="rms")
+            nc.scalar.activation(out=rms[:], in_=sumsq[:], func=ACT.Sqrt, bias=eps_col[:, 0:1], scale=1.0 / DH)
+            return vbanks, rms
+
+        def rotate(t, vbanks):
+            w1 = work.tile([P, BLOCKS, DH], F32, name="w1")
+            w2 = work.tile([P, BLOCKS, DH], F32, name="w2")
+            for j in range(BLOCKS // BANK_BLOCKS):
+                c = 0 if j < 2 else 1
+                bank = vbanks[j][:].rearrange("p (n d) -> p n d", d=DH)
+                blocks = slice(BANK_BLOCKS * j, BANK_BLOCKS * (j + 1))
+                nc.vector.tensor_tensor(
+                    out=w1[:, blocks, :], in0=bank,
+                    in1=a_tab[:, t, c, :].unsqueeze(1).to_broadcast([P, BANK_BLOCKS, DH]), op=ALU.mult,
+                )
+                nc.vector.tensor_tensor(
+                    out=w2[:, blocks, 0:HALF], in0=bank[:, :, HALF:DH],
+                    in1=b_tab[:, t, c, 0:HALF].unsqueeze(1).to_broadcast([P, BANK_BLOCKS, HALF]), op=ALU.mult,
+                )
+                nc.vector.tensor_tensor(
+                    out=w2[:, blocks, HALF:DH], in0=bank[:, :, 0:HALF],
+                    in1=b_tab[:, t, c, HALF:DH].unsqueeze(1).to_broadcast([P, BANK_BLOCKS, HALF]), op=ALU.mult,
+                )
+                nc.gpsimd.tensor_tensor(out=w1[:, blocks, :], in0=w1[:, blocks, :], in1=w2[:, blocks, :], op=ALU.add)
+            return w1
+
+        def rotate_shift(t):
+            shift_ps = psum.tile([P, 2, DH], F32, tag="shift", bufs=1, name="shift_ps")
+            nc.tensor.matmul(
+                out=shift_ps[:].rearrange("p c d -> p (c d)"), lhsT=trig_t[:, 0, t, :],
+                rhs=diag_shift[:].rearrange("p c d -> p (c d)"), start=True, stop=False,
+            )
+            nc.tensor.matmul(
+                out=shift_ps[:].rearrange("p c d -> p (c d)"), lhsT=trig_t[:, 1, t, :],
+                rhs=diag_shift_rot[:].rearrange("p c d -> p (c d)"), start=False, stop=True,
+            )
+            return shift_ps
+
+        def finish(t, w1, rstd, shift_ps):
+            if t % ST == 0:
+                out_tiles["q"] = stage.tile([P, B * H, ST, DH], F32, name="rq")
+                out_tiles["k"] = stage.tile([P, B, ST, DH], F32, name="rk")
+            rq = out_tiles["q"]
+            rk = out_tiles["k"]
+            for blk in range(BLOCKS):
+                is_q = blk < H * B
+                nc.vector.scalar_tensor_tensor(
+                    out=rq[:, blk, t % ST, :] if is_q else rk[:, blk - H * B, t % ST, :],
+                    in0=w1[:, blk, :], scalar=rstd[:, blk : blk + 1],
+                    in1=shift_ps[:, 0 if is_q else 1, :], op0=ALU.mult, op1=ALU.add,
+                )
+                if t % ST == ST - 1 and blk == H * B - 1:
+                    nc.sync.dma_start(out=q_view[:, :, t - ST + 1 : t + 1, :], in_=rq[:])
+            if t % ST == ST - 1:
+                nc.sync.dma_start(out=k_view[:, :, t - ST + 1 : t + 1, :], in_=rk[:])
+
+        grouped_of = {0: transpose_x(0)}
+        build_tables(nc.vector, 0)
+        mx_of = {0: quantise(grouped_of[0])}
+        build_tables(nc.vector, TABLE_T)
+        build_tables(nc.gpsimd, 2 * TABLE_T)
+        build_tables(nc.gpsimd, 3 * TABLE_T)
+        grouped_of[1] = transpose_x(1)
+        banks_of = {0: project(0, mx_of[0][0], mx_of[0][1])}
+
+        shift_rot = const.tile([P, 2, DH], BF16)
+        nc.vector.tensor_scalar_mul(out=shift_rot[:, :, 0:HALF], in0=par_b[:, 2:4, HALF:DH], scalar1=-1.0)
+        nc.vector.tensor_copy(out=shift_rot[:, :, HALF:DH], in_=par_b[:, 2:4, 0:HALF])
+        ident_pair = ident_bf[:].unsqueeze(1).to_broadcast([P, 2, P])
+        diag_shift = const.tile([P, 2, DH], BF16)
+        nc.vector.tensor_tensor(out=diag_shift[:], in0=ident_pair, in1=par_b[:, 2:4, :], op=ALU.mult)
+        diag_shift_rot = const.tile([P, 2, DH], BF16)
+        nc.vector.tensor_tensor(out=diag_shift_rot[:], in0=ident_pair, in1=shift_rot[:], op=ALU.mult)
+        trig_t = const.tile([P, 2, T, P], BF16)
+        for t0 in range(0, T, 8):
+            for i, trig in enumerate((cos_sb, sin_sb)):
+                tp = psum.tile([P, 8, P], BF16, tag="xt", name="tp")
+                for j in range(8):
+                    nc.tensor.transpose(tp[:, j, :], trig[:, t0 + j, :], ident_bf[:])
+                nc.scalar.copy(out=trig_t[:, i, t0 : t0 + 8, :], in_=tp[:])
+
+        w_of = {}
+        rstd_of = {}
+        shift_of = {}
+        for n in range(T + 1):
+            if n < T:
+                w_of[n] = rotate(n, banks_of[n][0])
+            if n + 1 < T:
+                mx_of[n + 1] = quantise(grouped_of[n + 1])
+            if n < T:
+                rstd_of[n] = work.tile([P, BLOCKS], F32, name="rstd")
+                nc.vector.reciprocal(out=rstd_of[n][:], in_=banks_of[n][1][:])
+            if n >= 1:
+                finish(n - 1, w_of[n - 1], rstd_of[n - 1], shift_of[n - 1])
+            if n + 2 < T:
+                grouped_of[n + 2] = transpose_x(n + 2)
+            if n + 1 < T:
+                banks_of[n + 1] = project(n + 1, mx_of[n + 1][0], mx_of[n + 1][1])
+            if n < T:
+                shift_of[n] = rotate_shift(n)

@@ -171,9 +171,9 @@ def tile_groupqueryattention_pa_t_kernel(
                 vb = psum.tile([P, BANK_BLOCKS * DH], F32, tag="vbank", bufs=3, name="vb")
                 vbanks.append(vb)
             for b in range(B):
-                pass_mx(vbanks[b // 2][:, (b % 2) * H * DH : (b % 2 + 1) * H * DH], b, 0, H * DH)
+                pass_mx(vbanks[0][:, b * DH : (b + 1) * DH], b, H * DH, (H + 1) * DH)
             for b in range(B):
-                pass_mx(vbanks[2][:, b * DH : (b + 1) * DH], b, H * DH, (H + 1) * DH)
+                pass_mx(vbanks[1 + b // 2][:, (b % 2) * H * DH : (b % 2 + 1) * H * DH], b, 0, H * DH)
             if t % ST == 0:
                 out_tiles["v"] = stage.tile([P, B, ST, DH], F32, name="rv")
             rv = out_tiles["v"]
@@ -183,7 +183,7 @@ def tile_groupqueryattention_pa_t_kernel(
                 pass_mx(sbank[:], b, 0, N_ALL)
                 nc.scalar.copy(out=rv[:, b, t % ST, :], in_=sbank[:, (H + 1) * DH : N_ALL])
                 for h in range(H + 1):
-                    blk = H * b + h if h < H else H * B + b
+                    blk = B + H * b + h if h < H else b
                     junk = work.tile([P, DH], F32, name="junk")
                     nc.scalar.activation(
                         out=junk[:], in_=sbank[:, h * DH : (h + 1) * DH], func=ACT.Square,
@@ -199,7 +199,7 @@ def tile_groupqueryattention_pa_t_kernel(
             w1 = work.tile([P, BLOCKS, DH], F32, name="w1")
             w2 = work.tile([P, BLOCKS, DH], F32, name="w2")
             for j in range(BLOCKS // BANK_BLOCKS):
-                c = 0 if j < 2 else 1
+                c = 1 if j == 0 else 0
                 bank = vbanks[j][:].rearrange("p (n d) -> p n d", d=DH)
                 blocks = slice(BANK_BLOCKS * j, BANK_BLOCKS * (j + 1))
                 nc.vector.tensor_tensor(
@@ -217,16 +217,13 @@ def tile_groupqueryattention_pa_t_kernel(
                 nc.gpsimd.tensor_tensor(out=w1[:, blocks, :], in0=w1[:, blocks, :], in1=w2[:, blocks, :], op=ALU.add)
             return w1
 
-        def rotate_shift(t):
-            shift_ps = psum.tile([P, 2, DH], F32, tag="shift", bufs=1, name="shift_ps")
-            nc.tensor.matmul(
-                out=shift_ps[:].rearrange("p c d -> p (c d)"), lhsT=trig_t[:, 0, t, :],
-                rhs=diag_shift[:].rearrange("p c d -> p (c d)"), start=True, stop=False,
-            )
-            nc.tensor.matmul(
-                out=shift_ps[:].rearrange("p c d -> p (c d)"), lhsT=trig_t[:, 1, t, :],
-                rhs=diag_shift_rot[:].rearrange("p c d -> p (c d)"), start=False, stop=True,
-            )
+        def rotate_shift(out, t, c):
+            nc.tensor.matmul(out=out, lhsT=trig_t[:, 0, t, :], rhs=diag_shift[:, c, :], start=True, stop=False)
+            nc.tensor.matmul(out=out, lhsT=trig_t[:, 1, t, :], rhs=diag_shift_rot[:, c, :], start=False, stop=True)
+
+        def rotate_shift_q(t):
+            shift_ps = psum.tile([P, DH], F32, tag="shift", bufs=1, name="shift_ps")
+            rotate_shift(shift_ps[:], t, 0)
             return shift_ps
 
         def finish(t, w1, rstd, shift_ps):
@@ -235,17 +232,22 @@ def tile_groupqueryattention_pa_t_kernel(
                 out_tiles["k"] = stage.tile([P, B, ST, DH], F32, name="rk")
             rq = out_tiles["q"]
             rk = out_tiles["k"]
-            for blk in range(BLOCKS):
-                is_q = blk < H * B
-                nc.vector.scalar_tensor_tensor(
-                    out=rq[:, blk, t % ST, :] if is_q else rk[:, blk - H * B, t % ST, :],
-                    in0=w1[:, blk, :], scalar=rstd[:, blk : blk + 1],
-                    in1=shift_ps[:, 0 if is_q else 1, :], op0=ALU.mult, op1=ALU.add,
-                )
-                if t % ST == ST - 1 and blk == H * B - 1:
-                    nc.sync.dma_start(out=q_view[:, :, t - ST + 1 : t + 1, :], in_=rq[:])
+            zk = work.tile([P, B, DH], F32, name="zk")
+            for b in range(B):
+                nc.scalar.activation(out=zk[:, b, :], in_=w1[:, b, :], func=ACT.Copy, scale=rstd[:, b : b + 1])
+            nc.gpsimd.tensor_tensor(
+                out=rk[:, :, t % ST, :], in0=zk[:],
+                in1=shift_k[:, t, :].unsqueeze(1).to_broadcast([P, B, DH]), op=ALU.add,
+            )
             if t % ST == ST - 1:
                 nc.sync.dma_start(out=k_view[:, :, t - ST + 1 : t + 1, :], in_=rk[:])
+            for i in range(B * H):
+                nc.vector.scalar_tensor_tensor(
+                    out=rq[:, i, t % ST, :], in0=w1[:, B + i, :], scalar=rstd[:, B + i : B + i + 1],
+                    in1=shift_ps[:], op0=ALU.mult, op1=ALU.add,
+                )
+            if t % ST == ST - 1:
+                nc.sync.dma_start(out=q_view[:, :, t - ST + 1 : t + 1, :], in_=rq[:])
 
         grouped_of = {0: transpose_x(0)}
         build_tables(nc.vector, 0)
@@ -271,6 +273,12 @@ def tile_groupqueryattention_pa_t_kernel(
                 for j in range(8):
                     nc.tensor.transpose(tp[:, j, :], trig[:, t0 + j, :], ident_bf[:])
                 nc.scalar.copy(out=trig_t[:, i, t0 : t0 + 8, :], in_=tp[:])
+        shift_k = const.tile([P, T, DH], F32)
+        for t0 in range(0, T, BANK_BLOCKS):
+            sk = psum.tile([P, BANK_BLOCKS, DH], F32, tag="xt", name="sk")
+            for j in range(BANK_BLOCKS):
+                rotate_shift(sk[:, j, :], t0 + j, 1)
+            nc.scalar.copy(out=shift_k[:, t0 : t0 + BANK_BLOCKS, :], in_=sk[:])
 
         w_of = {}
         rstd_of = {}
@@ -290,4 +298,4 @@ def tile_groupqueryattention_pa_t_kernel(
             if n + 1 < T:
                 banks_of[n + 1] = project(n + 1, mx_of[n + 1][0], mx_of[n + 1][1])
             if n < T:
-                shift_of[n] = rotate_shift(n)
+                shift_of[n] = rotate_shift_q(n)

@@ -24,8 +24,7 @@ T = S // P
 N_ALL = (H + 2) * DH
 BLOCKS = B * (H + 1)
 BANK_BLOCKS = 4
-ST = 2
-TABLE_T = 4
+CHUNK = 4
 
 FLOPS = 2 * B * S * D * N_ALL
 
@@ -51,6 +50,8 @@ def tile_groupqueryattention_pa_t_kernel(
 ):
     nc = tc.nc
     x_view = x.rearrange("b (p t) k -> p b t k", t=T)
+    cos_view = cos_thetas.rearrange("(p t) d -> p t d", t=T)
+    sin_view = sin_thetas.rearrange("(p t) d -> p t d", t=T)
     q_view = out_0.rearrange("b h (p t) d -> p (b h) t d", t=T)
     k_view = out_1.rearrange("b h (p t) d -> p (b h) t d", t=T)
     v_view = out_2.rearrange("b h (p t) d -> p (b h) t d", t=T)
@@ -61,19 +62,30 @@ def tile_groupqueryattention_pa_t_kernel(
         xpool = ctx.enter_context(tc.tile_pool(name="xpool", bufs=1))
         quant = ctx.enter_context(tc.tile_pool(name="quant", bufs=2))
         work = ctx.enter_context(tc.tile_pool(name="work", bufs=3))
-        stage = ctx.enter_context(tc.tile_pool(name="stage", bufs=2))
+        stage = ctx.enter_context(tc.tile_pool(name="stage", bufs=4))
         psum = ctx.enter_context(tc.psum_pool(name="psum", bufs=2))
 
         x_tiles = []
         for t in range(T):
-            xt_sb = xpool.tile([P, B, D], BF16, name="x%d" % t)
-            x_tiles.append(xt_sb)
+            x_sb = xpool.tile([P, B, D], BF16, name="x%d" % t)
+            x_tiles.append(x_sb)
 
         def load_x(t):
             nc.sync.dma_start(out=x_tiles[t][:], in_=x_view[:, :, t, :])
 
+        cos_sb = const.tile([P, T, DH], BF16)
+        sin_sb = const.tile([P, T, DH], BF16)
+
+        def load_trig(t0, t1):
+            nc.sync.dma_start(out=cos_sb[:, t0:t1, :], in_=cos_view[:, t0:t1, :])
+            nc.sync.dma_start(out=sin_sb[:, t0:t1, :], in_=sin_view[:, t0:t1, :])
+
+        par_b = const.tile([P, 4, DH], BF16)
+        for i, vec in enumerate((q_scale, k_scale, q_shift, k_shift)):
+            nc.scalar.dma_start(out=par_b[:, i, :], in_=vec.partition_broadcast(P))
+
         load_x(0)
-        load_x(1)
+        load_trig(0, T // 2)
         w_codes = const.tile([P, 4 * N_ALL], U8, align_bytes=64)
         w_scales = const.tile([P, N_ALL], U8, align_bytes=64)
         nc.vector.memset(w_scales[:].bitcast(I32), 0)
@@ -90,16 +102,10 @@ def tile_groupqueryattention_pa_t_kernel(
                     in_=scales[0, 4 * quad : 4 * quad + 4, :].bitcast(I32),
                 )
             col += n
+        load_x(1)
+        load_trig(T // 2, T)
         for t in range(2, T):
             load_x(t)
-
-        par_b = const.tile([P, 4, DH], BF16)
-        for i, vec in enumerate((q_scale, k_scale, q_shift, k_shift)):
-            nc.scalar.dma_start(out=par_b[:, i, :], in_=vec.partition_broadcast(P))
-        cos_sb = const.tile([P, T, DH], BF16)
-        sin_sb = const.tile([P, T, DH], BF16)
-        nc.scalar.dma_start(out=cos_sb[:], in_=cos_thetas.rearrange("(p t) d -> p t d", t=T))
-        nc.scalar.dma_start(out=sin_sb[:], in_=sin_thetas.rearrange("(p t) d -> p t d", t=T))
 
         ident_f32 = const.tile([P, P], F32)
         make_identity(nc, ident_f32[:])
@@ -110,11 +116,14 @@ def tile_groupqueryattention_pa_t_kernel(
         warm = const.tile([P, 1], F32)
         nc.scalar.activation(out=warm[:], in_=eps_col[:], func=ACT.Sqrt)
 
+        def rot(out, in_):
+            nc.vector.tensor_scalar_mul(out=out[:, :, 0:HALF], in0=in_[:, :, HALF:DH], scalar1=-1.0)
+            nc.vector.tensor_copy(out=out[:, :, HALF:DH], in_=in_[:, :, 0:HALF])
+
         gain = const.tile([P, 2, DH], F32)
         nc.vector.tensor_scalar_add(out=gain[:], in0=par_b[:, 0:2, :], scalar1=1.0)
         gain_rot = const.tile([P, 2, DH], F32)
-        nc.vector.tensor_scalar_mul(out=gain_rot[:, :, 0:HALF], in0=gain[:, :, HALF:DH], scalar1=-1.0)
-        nc.vector.tensor_copy(out=gain_rot[:, :, HALF:DH], in_=gain[:, :, 0:HALF])
+        rot(gain_rot, gain)
 
         a_tab = const.tile([P, T, 2, DH], F32)
         b_tab = const.tile([P, T, 2, DH], F32)
@@ -122,9 +131,9 @@ def tile_groupqueryattention_pa_t_kernel(
         def build_tables(engine, t0):
             for tab, trig, vec in ((a_tab, cos_sb, gain), (b_tab, sin_sb, gain_rot)):
                 engine.tensor_tensor(
-                    out=tab[:, t0 : t0 + TABLE_T, :, :],
-                    in0=trig[:, t0 : t0 + TABLE_T, :].unsqueeze(2).to_broadcast([P, TABLE_T, 2, DH]),
-                    in1=vec[:].unsqueeze(1).to_broadcast([P, TABLE_T, 2, DH]),
+                    out=tab[:, t0 : t0 + CHUNK, :, :],
+                    in0=trig[:, t0 : t0 + CHUNK, :].unsqueeze(2).to_broadcast([P, CHUNK, 2, DH]),
+                    in1=vec[:].unsqueeze(1).to_broadcast([P, CHUNK, 2, DH]),
                     op=ALU.mult,
                 )
 
@@ -152,8 +161,6 @@ def tile_groupqueryattention_pa_t_kernel(
             )
             return codes, planes
 
-        out_tiles = {}
-
         def project(t, codes, planes):
             def pass_mx(out, b, c0, c1):
                 nc.tensor.matmul_mx(
@@ -174,14 +181,12 @@ def tile_groupqueryattention_pa_t_kernel(
                 pass_mx(vbanks[0][:, b * DH : (b + 1) * DH], b, H * DH, (H + 1) * DH)
             for b in range(B):
                 pass_mx(vbanks[1 + b // 2][:, (b % 2) * H * DH : (b % 2 + 1) * H * DH], b, 0, H * DH)
-            if t % ST == 0:
-                out_tiles["v"] = stage.tile([P, B, ST, DH], F32, name="rv")
-            rv = out_tiles["v"]
+            rv = stage.tile([P, B, DH], F32, name="rv")
             sumsq = work.tile([P, BLOCKS], F32, name="sumsq")
             for b in range(B):
                 sbank = psum.tile([P, N_ALL], F32, tag="sbank", name="sbank")
                 pass_mx(sbank[:], b, 0, N_ALL)
-                nc.scalar.copy(out=rv[:, b, t % ST, :], in_=sbank[:, (H + 1) * DH : N_ALL])
+                nc.scalar.copy(out=rv[:, b, :], in_=sbank[:, (H + 1) * DH : N_ALL])
                 for h in range(H + 1):
                     blk = B + H * b + h if h < H else b
                     junk = work.tile([P, DH], F32, name="junk")
@@ -189,13 +194,12 @@ def tile_groupqueryattention_pa_t_kernel(
                         out=junk[:], in_=sbank[:, h * DH : (h + 1) * DH], func=ACT.Square,
                         accum_out=sumsq[:, blk : blk + 1],
                     )
-            if t % ST == ST - 1:
-                nc.sync.dma_start(out=v_view[:, :, t - ST + 1 : t + 1, :], in_=rv[:])
+            nc.sync.dma_start(out=v_view[:, :, t, :], in_=rv[:])
             rms = work.tile([P, BLOCKS], F32, name="rms")
             nc.scalar.activation(out=rms[:], in_=sumsq[:], func=ACT.Sqrt, bias=eps_col[:, 0:1], scale=1.0 / DH)
             return vbanks, rms
 
-        def rotate(t, vbanks):
+        def rotate(t, vbanks, adder):
             w1 = work.tile([P, BLOCKS, DH], F32, name="w1")
             w2 = work.tile([P, BLOCKS, DH], F32, name="w2")
             for j in range(BLOCKS // BANK_BLOCKS):
@@ -214,78 +218,82 @@ def tile_groupqueryattention_pa_t_kernel(
                     out=w2[:, blocks, HALF:DH], in0=bank[:, :, 0:HALF],
                     in1=b_tab[:, t, c, HALF:DH].unsqueeze(1).to_broadcast([P, BANK_BLOCKS, HALF]), op=ALU.mult,
                 )
-                nc.gpsimd.tensor_tensor(out=w1[:, blocks, :], in0=w1[:, blocks, :], in1=w2[:, blocks, :], op=ALU.add)
+            adder.tensor_tensor(out=w1[:], in0=w1[:], in1=w2[:], op=ALU.add)
             return w1
 
+        shift_rot = const.tile([P, 2, DH], BF16)
+        diag_shift = const.tile([P, 2, DH], BF16)
+        diag_shift_rot = const.tile([P, 2, DH], BF16)
+        trig_t = const.tile([P, T, 2, P], BF16)
+        shift_k = const.tile([P, T, DH], F32)
+
         def rotate_shift(out, t, c):
-            nc.tensor.matmul(out=out, lhsT=trig_t[:, 0, t, :], rhs=diag_shift[:, c, :], start=True, stop=False)
-            nc.tensor.matmul(out=out, lhsT=trig_t[:, 1, t, :], rhs=diag_shift_rot[:, c, :], start=False, stop=True)
+            nc.tensor.matmul(out=out, lhsT=trig_t[:, t, 0, :], rhs=diag_shift[:, c, :], start=True, stop=False)
+            nc.tensor.matmul(out=out, lhsT=trig_t[:, t, 1, :], rhs=diag_shift_rot[:, c, :], start=False, stop=True)
+
+        def transpose_trig(t0):
+            tp = psum.tile([P, CHUNK, 2, P], BF16, tag="xt", name="tp")
+            for j in range(CHUNK):
+                nc.tensor.transpose(tp[:, j, 0, :], cos_sb[:, t0 + j, :], ident_bf[:])
+                nc.tensor.transpose(tp[:, j, 1, :], sin_sb[:, t0 + j, :], ident_bf[:])
+            nc.scalar.copy(out=trig_t[:, t0 : t0 + CHUNK, :, :], in_=tp[:])
+
+        def rotate_shift_k(t0):
+            sk = psum.tile([P, CHUNK, DH], F32, tag="xt", name="sk")
+            for j in range(CHUNK):
+                rotate_shift(sk[:, j, :], t0 + j, 1)
+            nc.scalar.copy(out=shift_k[:, t0 : t0 + CHUNK, :], in_=sk[:])
 
         def rotate_shift_q(t):
-            shift_ps = psum.tile([P, DH], F32, tag="shift", bufs=1, name="shift_ps")
-            rotate_shift(shift_ps[:], t, 0)
-            return shift_ps
+            shift_q = psum.tile([P, DH], F32, tag="shift", bufs=1, name="shift_q")
+            rotate_shift(shift_q[:], t, 0)
+            return shift_q
 
-        def finish(t, w1, rstd, shift_ps):
-            if t % ST == 0:
-                out_tiles["q"] = stage.tile([P, B * H, ST, DH], F32, name="rq")
-                out_tiles["k"] = stage.tile([P, B, ST, DH], F32, name="rk")
-            rq = out_tiles["q"]
-            rk = out_tiles["k"]
-            zk = work.tile([P, B, DH], F32, name="zk")
-            for b in range(B):
-                nc.scalar.activation(out=zk[:, b, :], in_=w1[:, b, :], func=ACT.Copy, scale=rstd[:, b : b + 1])
-            nc.gpsimd.tensor_tensor(
-                out=rk[:, :, t % ST, :], in0=zk[:],
-                in1=shift_k[:, t, :].unsqueeze(1).to_broadcast([P, B, DH]), op=ALU.add,
-            )
-            if t % ST == ST - 1:
-                nc.sync.dma_start(out=k_view[:, :, t - ST + 1 : t + 1, :], in_=rk[:])
+        def finish(t, w1, rstd, shift_q):
+            rk = stage.tile([P, B, DH], F32, name="rk")
+            if t < T - 1:
+                zk = work.tile([P, B, DH], F32, name="zk")
+                for b in range(B):
+                    nc.scalar.activation(out=zk[:, b, :], in_=w1[:, b, :], func=ACT.Copy, scale=rstd[:, b : b + 1])
+                nc.gpsimd.tensor_tensor(
+                    out=rk[:], in0=zk[:], in1=shift_k[:, t, :].unsqueeze(1).to_broadcast([P, B, DH]), op=ALU.add,
+                )
+            else:
+                for b in range(B):
+                    nc.vector.scalar_tensor_tensor(
+                        out=rk[:, b, :], in0=w1[:, b, :], scalar=rstd[:, b : b + 1],
+                        in1=shift_k[:, t, :], op0=ALU.mult, op1=ALU.add,
+                    )
+            nc.sync.dma_start(out=k_view[:, :, t, :], in_=rk[:])
+            rq = stage.tile([P, B * H, DH], F32, name="rq")
             for i in range(B * H):
                 nc.vector.scalar_tensor_tensor(
-                    out=rq[:, i, t % ST, :], in0=w1[:, B + i, :], scalar=rstd[:, B + i : B + i + 1],
-                    in1=shift_ps[:], op0=ALU.mult, op1=ALU.add,
+                    out=rq[:, i, :], in0=w1[:, B + i, :], scalar=rstd[:, B + i : B + i + 1],
+                    in1=shift_q[:], op0=ALU.mult, op1=ALU.add,
                 )
-            if t % ST == ST - 1:
-                nc.sync.dma_start(out=q_view[:, :, t - ST + 1 : t + 1, :], in_=rq[:])
+            nc.sync.dma_start(out=q_view[:, :, t, :], in_=rq[:])
 
         grouped_of = {0: transpose_x(0)}
         build_tables(nc.vector, 0)
         mx_of = {0: quantise(grouped_of[0])}
-        build_tables(nc.vector, TABLE_T)
-        build_tables(nc.gpsimd, 2 * TABLE_T)
-        build_tables(nc.gpsimd, 3 * TABLE_T)
+        build_tables(nc.vector, CHUNK)
+        build_tables(nc.gpsimd, 2 * CHUNK)
+        build_tables(nc.gpsimd, 3 * CHUNK)
         grouped_of[1] = transpose_x(1)
+        transpose_trig(0)
         banks_of = {0: project(0, mx_of[0][0], mx_of[0][1])}
-
-        shift_rot = const.tile([P, 2, DH], BF16)
-        nc.vector.tensor_scalar_mul(out=shift_rot[:, :, 0:HALF], in0=par_b[:, 2:4, HALF:DH], scalar1=-1.0)
-        nc.vector.tensor_copy(out=shift_rot[:, :, HALF:DH], in_=par_b[:, 2:4, 0:HALF])
+        rot(shift_rot, par_b[:, 2:4, :])
         ident_pair = ident_bf[:].unsqueeze(1).to_broadcast([P, 2, P])
-        diag_shift = const.tile([P, 2, DH], BF16)
         nc.vector.tensor_tensor(out=diag_shift[:], in0=ident_pair, in1=par_b[:, 2:4, :], op=ALU.mult)
-        diag_shift_rot = const.tile([P, 2, DH], BF16)
         nc.vector.tensor_tensor(out=diag_shift_rot[:], in0=ident_pair, in1=shift_rot[:], op=ALU.mult)
-        trig_t = const.tile([P, 2, T, P], BF16)
-        for t0 in range(0, T, 8):
-            for i, trig in enumerate((cos_sb, sin_sb)):
-                tp = psum.tile([P, 8, P], BF16, tag="xt", name="tp")
-                for j in range(8):
-                    nc.tensor.transpose(tp[:, j, :], trig[:, t0 + j, :], ident_bf[:])
-                nc.scalar.copy(out=trig_t[:, i, t0 : t0 + 8, :], in_=tp[:])
-        shift_k = const.tile([P, T, DH], F32)
-        for t0 in range(0, T, BANK_BLOCKS):
-            sk = psum.tile([P, BANK_BLOCKS, DH], F32, tag="xt", name="sk")
-            for j in range(BANK_BLOCKS):
-                rotate_shift(sk[:, j, :], t0 + j, 1)
-            nc.scalar.copy(out=shift_k[:, t0 : t0 + BANK_BLOCKS, :], in_=sk[:])
+        rotate_shift_k(0)
 
         w_of = {}
         rstd_of = {}
         shift_of = {}
         for n in range(T + 1):
             if n < T:
-                w_of[n] = rotate(n, banks_of[n][0])
+                w_of[n] = rotate(n, banks_of[n][0], nc.gpsimd if n < T - 1 else nc.vector)
             if n + 1 < T:
                 mx_of[n + 1] = quantise(grouped_of[n + 1])
             if n < T:
@@ -299,3 +307,7 @@ def tile_groupqueryattention_pa_t_kernel(
                 banks_of[n + 1] = project(n + 1, mx_of[n + 1][0], mx_of[n + 1][1])
             if n < T:
                 shift_of[n] = rotate_shift_q(n)
+            if n % CHUNK == 1 and n + CHUNK - 1 < T:
+                transpose_trig(n + CHUNK - 1)
+            if n % CHUNK == 2 and n + CHUNK - 2 < T:
+                rotate_shift_k(n + CHUNK - 2)

@@ -122,18 +122,24 @@ def tile_groupqueryattention_pa_t_kernel(
 
         gain = const.tile([P, 2, DH], F32)
         nc.vector.tensor_scalar_add(out=gain[:], in0=par_b[:, 0:2, :], scalar1=1.0)
-        gain_rot = const.tile([P, 2, DH], F32)
-        rot(gain_rot, gain)
+        gain_sign = const.tile([P, 2, DH], F32)
+        nc.vector.tensor_copy(out=gain_sign[:, :, 0:HALF], in_=gain[:, :, 0:HALF])
+        nc.vector.tensor_scalar_mul(out=gain_sign[:, :, HALF:DH], in0=gain[:, :, HALF:DH], scalar1=-1.0)
 
-        a_tab = const.tile([P, T, 2, DH], F32)
-        b_tab = const.tile([P, T, 2, DH], F32)
+        tab = const.tile([P, T, 2, 2, DH], F32)
 
         def build_tables(engine, t0):
-            for tab, trig, vec in ((a_tab, cos_sb, gain), (b_tab, sin_sb, gain_rot)):
+            engine.tensor_tensor(
+                out=tab[:, t0 : t0 + CHUNK, :, 0, :],
+                in0=cos_sb[:, t0 : t0 + CHUNK, :].unsqueeze(2).to_broadcast([P, CHUNK, 2, DH]),
+                in1=gain[:].unsqueeze(1).to_broadcast([P, CHUNK, 2, DH]),
+                op=ALU.mult,
+            )
+            for lo, other in ((0, HALF), (HALF, 0)):
                 engine.tensor_tensor(
-                    out=tab[:, t0 : t0 + CHUNK, :, :],
-                    in0=trig[:, t0 : t0 + CHUNK, :].unsqueeze(2).to_broadcast([P, CHUNK, 2, DH]),
-                    in1=vec[:].unsqueeze(1).to_broadcast([P, CHUNK, 2, DH]),
+                    out=tab[:, t0 : t0 + CHUNK, :, 1, lo : lo + HALF],
+                    in0=sin_sb[:, t0 : t0 + CHUNK, other : other + HALF].unsqueeze(2).to_broadcast([P, CHUNK, 2, HALF]),
+                    in1=gain_sign[:, :, lo : lo + HALF].unsqueeze(1).to_broadcast([P, CHUNK, 2, HALF]),
                     op=ALU.mult,
                 )
 
@@ -200,25 +206,21 @@ def tile_groupqueryattention_pa_t_kernel(
             return vbanks, rms
 
         def rotate(t, vbanks, adder):
-            w1 = work.tile([P, BLOCKS, DH], F32, name="w1")
-            w2 = work.tile([P, BLOCKS, DH], F32, name="w2")
+            prod = work.tile([P, 2, BLOCKS, DH], F32, name="prod")
             for j in range(BLOCKS // BANK_BLOCKS):
                 c = 1 if j == 0 else 0
-                bank = vbanks[j][:].rearrange("p (n d) -> p n d", d=DH)
-                blocks = slice(BANK_BLOCKS * j, BANK_BLOCKS * (j + 1))
                 nc.vector.tensor_tensor(
-                    out=w1[:, blocks, :], in0=bank,
-                    in1=a_tab[:, t, c, :].unsqueeze(1).to_broadcast([P, BANK_BLOCKS, DH]), op=ALU.mult,
+                    out=prod[:, :, BANK_BLOCKS * j : BANK_BLOCKS * (j + 1), :],
+                    in0=vbanks[j][:].rearrange("p (n d) -> p n d", d=DH).unsqueeze(1).to_broadcast([P, 2, BANK_BLOCKS, DH]),
+                    in1=tab[:, t, c, :, :].unsqueeze(2).to_broadcast([P, 2, BANK_BLOCKS, DH]),
+                    op=ALU.mult,
                 )
-                nc.vector.tensor_tensor(
-                    out=w2[:, blocks, 0:HALF], in0=bank[:, :, HALF:DH],
-                    in1=b_tab[:, t, c, 0:HALF].unsqueeze(1).to_broadcast([P, BANK_BLOCKS, HALF]), op=ALU.mult,
-                )
-                nc.vector.tensor_tensor(
-                    out=w2[:, blocks, HALF:DH], in0=bank[:, :, 0:HALF],
-                    in1=b_tab[:, t, c, HALF:DH].unsqueeze(1).to_broadcast([P, BANK_BLOCKS, HALF]), op=ALU.mult,
-                )
-            adder.tensor_tensor(out=w1[:], in0=w1[:], in1=w2[:], op=ALU.add)
+            w1 = prod[:, 0, :, :]
+            halves = "p n (h d) -> p n h d"
+            adder.tensor_tensor(
+                out=w1.rearrange(halves, h=2), in0=w1.rearrange(halves, h=2),
+                in1=prod[:, 1, :, :].rearrange(halves, h=2)[:, :, ::-1, :], op=ALU.add,
+            )
             return w1
 
         shift_rot = const.tile([P, 2, DH], BF16)

@@ -80,9 +80,12 @@ def tile_groupqueryattention_pa_t_kernel(
             nc.sync.dma_start(out=cos_sb[:, t0:t1, :], in_=cos_view[:, t0:t1, :])
             nc.sync.dma_start(out=sin_sb[:, t0:t1, :], in_=sin_view[:, t0:t1, :])
 
-        par_b = const.tile([P, 4, DH], BF16)
+        par_rows = const.tile([P, 4 * DH], BF16)
+        nc.vector.memset(par_rows[:], 0.0)
         for i, vec in enumerate((q_scale, k_scale, q_shift, k_shift)):
-            nc.scalar.dma_start(out=par_b[:, i, :], in_=vec.partition_broadcast(P))
+            nc.scalar.dma_start(out=par_rows[0:1, i * DH : (i + 1) * DH], in_=vec.rearrange("(o d) -> o d", o=1))
+        ones_bf = const.tile([P, P], BF16)
+        nc.vector.memset(ones_bf[:], 1.0)
 
         load_x(0)
         load_trig(0, T // 2)
@@ -114,7 +117,11 @@ def tile_groupqueryattention_pa_t_kernel(
         eps_col = const.tile([P, 1], F32)
         nc.vector.memset(eps_col[:], EPS)
         warm = const.tile([P, 1], F32)
-        nc.scalar.activation(out=warm[:], in_=eps_col[:], func=ACT.Sqrt)
+        nc.scalar.activation(out=warm[:], in_=eps_col[:], func=ACT.Abs_reciprocal_sqrt)
+        par_ps = psum.tile([P, 4 * DH], F32, tag="shift", bufs=1, name="par_ps")
+        nc.tensor.matmul(out=par_ps[:], lhsT=ones_bf[:], rhs=par_rows[:], start=True, stop=True)
+        par_b = const.tile([P, 4, DH], BF16)
+        nc.vector.tensor_copy(out=par_b[:].rearrange("p i d -> p (i d)"), in_=par_ps[:])
 
         def rot(out, in_):
             nc.vector.tensor_scalar_mul(out=out[:, :, 0:HALF], in0=in_[:, :, HALF:DH], scalar1=-1.0)
@@ -158,8 +165,8 @@ def tile_groupqueryattention_pa_t_kernel(
             return grouped
 
         def quantise(grouped):
-            codes = quant.tile([P, B * P], U32, align_bytes=64, name="codes")
-            planes = quant.tile([P, B * P], U8, align_bytes=64, name="planes")
+            codes = quant.tile([P, B * P], U32, align_bytes=64, bufs=3, name="codes")
+            planes = quant.tile([P, B * P], U8, align_bytes=64, bufs=3, name="planes")
             nc.vector.quantize_mx(
                 out=codes[:].bitcast(FP8X4),
                 scales=planes[:],
@@ -187,23 +194,33 @@ def tile_groupqueryattention_pa_t_kernel(
                 pass_mx(vbanks[0][:, b * DH : (b + 1) * DH], b, H * DH, (H + 1) * DH)
             for b in range(B):
                 pass_mx(vbanks[1 + b // 2][:, (b % 2) * H * DH : (b % 2 + 1) * H * DH], b, 0, H * DH)
-            rv = stage.tile([P, B, DH], F32, name="rv")
             sumsq = work.tile([P, BLOCKS], F32, name="sumsq")
-            for b in range(B):
-                sbank = psum.tile([P, N_ALL], F32, tag="sbank", name="sbank")
-                pass_mx(sbank[:], b, 0, N_ALL)
-                nc.scalar.copy(out=rv[:, b, :], in_=sbank[:, (H + 1) * DH : N_ALL])
-                for h in range(H + 1):
-                    blk = B + H * b + h if h < H else b
+            for j in range(BLOCKS // BANK_BLOCKS):
+                sbank = psum.tile([P, BANK_BLOCKS * DH], F32, tag="sbank", name="sbank")
+                if j == 0:
+                    for b in range(B):
+                        pass_mx(sbank[:, b * DH : (b + 1) * DH], b, H * DH, (H + 1) * DH)
+                else:
+                    for i in range(2):
+                        pass_mx(sbank[:, i * H * DH : (i + 1) * H * DH], 2 * (j - 1) + i, 0, H * DH)
+                for i in range(BANK_BLOCKS):
+                    blk = BANK_BLOCKS * j + i
                     junk = work.tile([P, DH], F32, name="junk")
                     nc.scalar.activation(
-                        out=junk[:], in_=sbank[:, h * DH : (h + 1) * DH], func=ACT.Square,
+                        out=junk[:], in_=sbank[:, i * DH : (i + 1) * DH], func=ACT.Square,
                         accum_out=sumsq[:, blk : blk + 1],
                     )
+            rstd = work.tile([P, BLOCKS], F32, name="rstd")
+            nc.scalar.activation(
+                out=rstd[:], in_=sumsq[:], func=ACT.Abs_reciprocal_sqrt, bias=eps_col[:, 0:1], scale=1.0 / DH
+            )
+            vv = psum.tile([P, B * DH], F32, tag="sbank", name="vv")
+            for b in range(B):
+                pass_mx(vv[:, b * DH : (b + 1) * DH], b, (H + 1) * DH, N_ALL)
+            rv = stage.tile([P, B, DH], F32, name="rv")
+            nc.scalar.copy(out=rv[:].rearrange("p b d -> p (b d)"), in_=vv[:])
             nc.sync.dma_start(out=v_view[:, :, t, :], in_=rv[:])
-            rms = work.tile([P, BLOCKS], F32, name="rms")
-            nc.scalar.activation(out=rms[:], in_=sumsq[:], func=ACT.Sqrt, bias=eps_col[:, 0:1], scale=1.0 / DH)
-            return vbanks, rms
+            return vbanks, rstd
 
         def rotate(t, vbanks, adder):
             prod = work.tile([P, 2, BLOCKS, DH], F32, name="prod")
@@ -289,6 +306,8 @@ def tile_groupqueryattention_pa_t_kernel(
         nc.vector.tensor_tensor(out=diag_shift[:], in0=ident_pair, in1=par_b[:, 2:4, :], op=ALU.mult)
         nc.vector.tensor_tensor(out=diag_shift_rot[:], in0=ident_pair, in1=shift_rot[:], op=ALU.mult)
         rotate_shift_k(0)
+        mx_of[1] = quantise(grouped_of[1])
+        grouped_of[2] = transpose_x(2)
 
         w_of = {}
         rstd_of = {}
@@ -296,15 +315,14 @@ def tile_groupqueryattention_pa_t_kernel(
         for n in range(T + 1):
             if n < T:
                 w_of[n] = rotate(n, banks_of[n][0], nc.gpsimd if n < T - 1 else nc.vector)
-            if n + 1 < T:
-                mx_of[n + 1] = quantise(grouped_of[n + 1])
+            if n + 2 < T:
+                mx_of[n + 2] = quantise(grouped_of[n + 2])
             if n < T:
-                rstd_of[n] = work.tile([P, BLOCKS], F32, name="rstd")
-                nc.vector.reciprocal(out=rstd_of[n][:], in_=banks_of[n][1][:])
+                rstd_of[n] = banks_of[n][1]
             if n >= 1:
                 finish(n - 1, w_of[n - 1], rstd_of[n - 1], shift_of[n - 1])
-            if n + 2 < T:
-                grouped_of[n + 2] = transpose_x(n + 2)
+            if n + 3 < T:
+                grouped_of[n + 3] = transpose_x(n + 3)
             if n + 1 < T:
                 banks_of[n + 1] = project(n + 1, mx_of[n + 1][0], mx_of[n + 1][1])
             if n < T:

@@ -151,16 +151,22 @@ def tile_groupqueryattention_pa_t_kernel(
                 )
 
         def transpose_x(t):
-            grouped = quant.tile([P, B, P, 2], F32, align_bytes=64, name="grouped")
+            banks = []
             for j in range(B // 2):
                 xt = psum.tile([P, 2, 2, P], F32, tag="xt", name="xt")
                 for i in range(2):
                     x_words = x_tiles[t][:, 2 * j + i, :].bitcast(F32)
                     for u in range(2):
                         nc.tensor.transpose(xt[:, i, u, :], x_words[:, u : D // 2 : 2], ident_f32[:])
+                banks.append(xt)
+            return banks
+
+        def group_x(banks):
+            grouped = quant.tile([P, B, P, 2], F32, align_bytes=64, name="grouped")
+            for j in range(B // 2):
                 nc.scalar.copy(
                     out=grouped[:, 2 * j : 2 * j + 2, :, :],
-                    in_=xt[:].rearrange("p i u r -> p i r u"),
+                    in_=banks[j][:].rearrange("p i u r -> p i r u"),
                 )
             return grouped
 
@@ -174,71 +180,63 @@ def tile_groupqueryattention_pa_t_kernel(
             )
             return codes, planes
 
-        def project(t, codes, planes):
-            def pass_mx(out, b, c0, c1):
-                nc.tensor.matmul_mx(
-                    out=out,
-                    lhsT=codes[:, b * P : (b + 1) * P].bitcast(FP8X4),
-                    lhsT_scale=planes[:, b * P : (b + 1) * P],
-                    rhs=w_codes[:, 4 * c0 : 4 * c1].bitcast(FP8X4),
-                    rhs_scale=w_scales[:, c0:c1],
-                    start=True,
-                    stop=True,
-                )
-
-            vbanks = []
-            for j in range(BLOCKS // BANK_BLOCKS):
-                vb = psum.tile([P, BANK_BLOCKS * DH], F32, tag="vbank", bufs=3, name="vb")
-                vbanks.append(vb)
-            for b in range(B):
-                pass_mx(vbanks[0][:, b * DH : (b + 1) * DH], b, H * DH, (H + 1) * DH)
-            for b in range(B):
-                pass_mx(vbanks[1 + b // 2][:, (b % 2) * H * DH : (b % 2 + 1) * H * DH], b, 0, H * DH)
-            sumsq = work.tile([P, BLOCKS], F32, name="sumsq")
-            for j in range(BLOCKS // BANK_BLOCKS):
-                sbank = psum.tile([P, BANK_BLOCKS * DH], F32, tag="sbank", name="sbank")
-                if j == 0:
-                    for b in range(B):
-                        pass_mx(sbank[:, b * DH : (b + 1) * DH], b, H * DH, (H + 1) * DH)
-                else:
-                    for i in range(2):
-                        pass_mx(sbank[:, i * H * DH : (i + 1) * H * DH], 2 * (j - 1) + i, 0, H * DH)
-                for i in range(BANK_BLOCKS):
-                    blk = BANK_BLOCKS * j + i
-                    junk = work.tile([P, DH], F32, name="junk")
-                    nc.scalar.activation(
-                        out=junk[:], in_=sbank[:, i * DH : (i + 1) * DH], func=ACT.Square,
-                        accum_out=sumsq[:, blk : blk + 1],
-                    )
-            rstd = work.tile([P, BLOCKS], F32, name="rstd")
-            nc.scalar.activation(
-                out=rstd[:], in_=sumsq[:], func=ACT.Abs_reciprocal_sqrt, bias=eps_col[:, 0:1], scale=1.0 / DH
+        def pass_x(out, mx, b, c0, c1):
+            nc.tensor.matmul_mx(
+                out=out,
+                lhsT=mx[0][:, b * P : (b + 1) * P].bitcast(FP8X4),
+                lhsT_scale=mx[1][:, b * P : (b + 1) * P],
+                rhs=w_codes[:, 4 * c0 : 4 * c1].bitcast(FP8X4),
+                rhs_scale=w_scales[:, c0:c1],
+                start=True,
+                stop=True,
             )
-            vv = psum.tile([P, B * DH], F32, tag="sbank", name="vv")
-            for b in range(B):
-                pass_mx(vv[:, b * DH : (b + 1) * DH], b, (H + 1) * DH, N_ALL)
-            rv = stage.tile([P, B, DH], F32, name="rv")
-            nc.scalar.copy(out=rv[:].rearrange("p b d -> p (b d)"), in_=vv[:])
-            nc.sync.dma_start(out=v_view[:, :, t, :], in_=rv[:])
-            return vbanks, rstd
 
-        def rotate(t, vbanks, adder):
+        def project(mx):
+            banks = []
+            for j in range(4):
+                ub = psum.tile([P, BANK_BLOCKS * DH], F32, tag="ubank", bufs=5, name="ub")
+                if j == 1 or j == 2:
+                    for i in range(2):
+                        pass_x(ub[:, i * H * DH : (i + 1) * H * DH], mx, 2 * (j - 1) + i, 0, H * DH)
+                else:
+                    c0 = H * DH if j == 0 else (H + 1) * DH
+                    for b in range(B):
+                        pass_x(ub[:, b * DH : (b + 1) * DH], mx, b, c0, c0 + DH)
+                banks.append(ub)
+            return banks
+
+        def rotate(t, banks, adder):
             prod = work.tile([P, 2, BLOCKS, DH], F32, name="prod")
+            sumsq = work.tile([P, BLOCKS], F32, name="sumsq")
             for j in range(BLOCKS // BANK_BLOCKS):
                 c = 1 if j == 0 else 0
                 nc.vector.tensor_tensor(
                     out=prod[:, :, BANK_BLOCKS * j : BANK_BLOCKS * (j + 1), :],
-                    in0=vbanks[j][:].rearrange("p (n d) -> p n d", d=DH).unsqueeze(1).to_broadcast([P, 2, BANK_BLOCKS, DH]),
+                    in0=banks[j][:].rearrange("p (n d) -> p n d", d=DH).unsqueeze(1).to_broadcast([P, 2, BANK_BLOCKS, DH]),
                     in1=tab[:, t, c, :, :].unsqueeze(2).to_broadcast([P, 2, BANK_BLOCKS, DH]),
                     op=ALU.mult,
                 )
+                for i in range(BANK_BLOCKS):
+                    blk = BANK_BLOCKS * j + i
+                    junk = work.tile([P, DH], F32, name="junk")
+                    nc.scalar.activation(
+                        out=junk[:], in_=banks[j][:, i * DH : (i + 1) * DH], func=ACT.Square,
+                        accum_out=sumsq[:, blk : blk + 1],
+                    )
             w1 = prod[:, 0, :, :]
             halves = "p n (h d) -> p n h d"
             adder.tensor_tensor(
                 out=w1.rearrange(halves, h=2), in0=w1.rearrange(halves, h=2),
                 in1=prod[:, 1, :, :].rearrange(halves, h=2)[:, :, ::-1, :], op=ALU.add,
             )
-            return w1
+            rstd = work.tile([P, BLOCKS], F32, name="rstd")
+            nc.scalar.activation(
+                out=rstd[:], in_=sumsq[:], func=ACT.Abs_reciprocal_sqrt, bias=eps_col[:, 0:1], scale=1.0 / DH
+            )
+            rv = stage.tile([P, B, DH], F32, name="rv")
+            nc.scalar.copy(out=rv[:].rearrange("p b d -> p (b d)"), in_=banks[3][:])
+            nc.sync.dma_start(out=v_view[:, :, t, :], in_=rv[:])
+            return w1, rstd
 
         shift_rot = const.tile([P, 2, DH], BF16)
         diag_shift = const.tile([P, 2, DH], BF16)
@@ -292,39 +290,38 @@ def tile_groupqueryattention_pa_t_kernel(
                 )
             nc.sync.dma_start(out=q_view[:, :, t, :], in_=rq[:])
 
-        grouped_of = {0: transpose_x(0)}
+        grouped_of = {0: group_x(transpose_x(0))}
         build_tables(nc.vector, 0)
         mx_of = {0: quantise(grouped_of[0])}
         build_tables(nc.vector, CHUNK)
         build_tables(nc.gpsimd, 2 * CHUNK)
         build_tables(nc.gpsimd, 3 * CHUNK)
-        grouped_of[1] = transpose_x(1)
+        grouped_of[1] = group_x(transpose_x(1))
         transpose_trig(0)
-        banks_of = {0: project(0, mx_of[0][0], mx_of[0][1])}
+        banks_of = {0: project(mx_of[0])}
         rot(shift_rot, par_b[:, 2:4, :])
         ident_pair = ident_bf[:].unsqueeze(1).to_broadcast([P, 2, P])
         nc.vector.tensor_tensor(out=diag_shift[:], in0=ident_pair, in1=par_b[:, 2:4, :], op=ALU.mult)
         nc.vector.tensor_tensor(out=diag_shift_rot[:], in0=ident_pair, in1=shift_rot[:], op=ALU.mult)
         rotate_shift_k(0)
         mx_of[1] = quantise(grouped_of[1])
-        grouped_of[2] = transpose_x(2)
+        grouped_of[2] = group_x(transpose_x(2))
 
-        w_of = {}
-        rstd_of = {}
+        done_of = {}
         shift_of = {}
         for n in range(T + 1):
+            if n + 3 < T:
+                xt_banks = transpose_x(n + 3)
             if n < T:
-                w_of[n] = rotate(n, banks_of[n][0], nc.gpsimd if n < T - 1 else nc.vector)
+                done_of[n] = rotate(n, banks_of[n], nc.gpsimd if n < T - 1 else nc.vector)
+            if n + 3 < T:
+                grouped_of[n + 3] = group_x(xt_banks)
             if n + 2 < T:
                 mx_of[n + 2] = quantise(grouped_of[n + 2])
-            if n < T:
-                rstd_of[n] = banks_of[n][1]
             if n >= 1:
-                finish(n - 1, w_of[n - 1], rstd_of[n - 1], shift_of[n - 1])
-            if n + 3 < T:
-                grouped_of[n + 3] = transpose_x(n + 3)
+                finish(n - 1, done_of[n - 1][0], done_of[n - 1][1], shift_of[n - 1])
             if n + 1 < T:
-                banks_of[n + 1] = project(n + 1, mx_of[n + 1][0], mx_of[n + 1][1])
+                banks_of[n + 1] = project(mx_of[n + 1])
             if n < T:
                 shift_of[n] = rotate_shift_q(n)
             if n % CHUNK == 1 and n + CHUNK - 1 < T:

@@ -87,8 +87,9 @@ def tile_groupqueryattention_pa_t_kernel(
         ones_bf = const.tile([P, P], BF16)
         nc.vector.memset(ones_bf[:], 1.0)
 
+        load_trig(0, CHUNK)
         load_x(0)
-        load_trig(0, T // 2)
+        load_trig(CHUNK, T)
         w_codes = const.tile([P, 4 * N_ALL], U8, align_bytes=64)
         w_scales = const.tile([P, N_ALL], U8, align_bytes=64)
         nc.vector.memset(w_scales[:].bitcast(I32), 0)
@@ -106,7 +107,6 @@ def tile_groupqueryattention_pa_t_kernel(
                 )
             col += n
         load_x(1)
-        load_trig(T // 2, T)
         for t in range(2, T):
             load_x(t)
 
@@ -283,12 +283,14 @@ def tile_groupqueryattention_pa_t_kernel(
                     )
             nc.sync.dma_start(out=k_view[:, :, t, :], in_=rk[:])
             rq = stage.tile([P, B * H, DH], F32, name="rq")
+            step = B * H // 2 if t == T - 1 else B * H
             for i in range(B * H):
                 nc.vector.scalar_tensor_tensor(
                     out=rq[:, i, :], in0=w1[:, B + i, :], scalar=rstd[:, B + i : B + i + 1],
                     in1=shift_q[:], op0=ALU.mult, op1=ALU.add,
                 )
-            nc.sync.dma_start(out=q_view[:, :, t, :], in_=rq[:])
+                if (i + 1) % step == 0:
+                    nc.sync.dma_start(out=q_view[:, i + 1 - step : i + 1, t, :], in_=rq[:, i + 1 - step : i + 1, :])
 
         grouped_of = {0: group_x(transpose_x(0))}
         build_tables(nc.vector, 0)

@@ -25,6 +25,7 @@ N_ALL = (H + 2) * DH
 BLOCKS = B * (H + 1)
 BANK_BLOCKS = 4
 CHUNK = 4
+K_ON_VECTOR = 1
 
 FLOPS = 2 * B * S * D * N_ALL
 
@@ -262,32 +263,41 @@ def tile_groupqueryattention_pa_t_kernel(
             nc.scalar.copy(out=shift_k[:, t0 : t0 + CHUNK, :], in_=sk[:])
 
         def rotate_shift_q(t):
-            shift_q = psum.tile([P, DH], F32, tag="shift", bufs=1, name="shift_q")
-            rotate_shift(shift_q[:], t, 0)
+            shift_q = psum.tile([P, 2, DH], F32, tag="shift", bufs=1, name="shift_q")
+            both = "p c d -> p (c d)"
+            nc.tensor.matmul(
+                out=shift_q[:].rearrange(both), lhsT=trig_t[:, t, 0, :], rhs=diag_shift[:].rearrange(both),
+                start=True, stop=False,
+            )
+            nc.tensor.matmul(
+                out=shift_q[:].rearrange(both), lhsT=trig_t[:, t, 1, :], rhs=diag_shift_rot[:].rearrange(both),
+                start=False, stop=True,
+            )
             return shift_q
 
         def finish(t, w1, rstd, shift_q):
             rk = stage.tile([P, B, DH], F32, name="rk")
-            if t < T - 1:
+            on_vector = K_ON_VECTOR if t < T - 1 else B
+            for b in range(on_vector):
+                nc.vector.scalar_tensor_tensor(
+                    out=rk[:, b, :], in0=w1[:, b, :], scalar=rstd[:, b : b + 1],
+                    in1=shift_q[:, 1, :], op0=ALU.mult, op1=ALU.add,
+                )
+            if on_vector < B:
                 zk = work.tile([P, B, DH], F32, name="zk")
-                for b in range(B):
+                for b in range(on_vector, B):
                     nc.scalar.activation(out=zk[:, b, :], in_=w1[:, b, :], func=ACT.Copy, scale=rstd[:, b : b + 1])
                 nc.gpsimd.tensor_tensor(
-                    out=rk[:], in0=zk[:], in1=shift_k[:, t, :].unsqueeze(1).to_broadcast([P, B, DH]), op=ALU.add,
+                    out=rk[:, on_vector:B, :], in0=zk[:, on_vector:B, :],
+                    in1=shift_k[:, t, :].unsqueeze(1).to_broadcast([P, B - on_vector, DH]), op=ALU.add,
                 )
-            else:
-                for b in range(B):
-                    nc.vector.scalar_tensor_tensor(
-                        out=rk[:, b, :], in0=w1[:, b, :], scalar=rstd[:, b : b + 1],
-                        in1=shift_k[:, t, :], op0=ALU.mult, op1=ALU.add,
-                    )
             nc.sync.dma_start(out=k_view[:, :, t, :], in_=rk[:])
             rq = stage.tile([P, B * H, DH], F32, name="rq")
             step = B * H // 2 if t == T - 1 else B * H
             for i in range(B * H):
                 nc.vector.scalar_tensor_tensor(
                     out=rq[:, i, :], in0=w1[:, B + i, :], scalar=rstd[:, B + i : B + i + 1],
-                    in1=shift_q[:], op0=ALU.mult, op1=ALU.add,
+                    in1=shift_q[:, 0, :], op0=ALU.mult, op1=ALU.add,
                 )
                 if (i + 1) % step == 0:
                     nc.sync.dma_start(out=q_view[:, i + 1 - step : i + 1, t, :], in_=rq[:, i + 1 - step : i + 1, :])

@@ -81,12 +81,9 @@ def tile_groupqueryattention_pa_t_kernel(
             nc.sync.dma_start(out=cos_sb[:, t0:t1, :], in_=cos_view[:, t0:t1, :])
             nc.sync.dma_start(out=sin_sb[:, t0:t1, :], in_=sin_view[:, t0:t1, :])
 
-        par_rows = const.tile([P, 4 * DH], BF16)
-        nc.vector.memset(par_rows[:], 0.0)
+        par_b = const.tile([P, 4, DH], BF16)
         for i, vec in enumerate((q_scale, k_scale, q_shift, k_shift)):
-            nc.scalar.dma_start(out=par_rows[0:1, i * DH : (i + 1) * DH], in_=vec.rearrange("(o d) -> o d", o=1))
-        ones_bf = const.tile([P, P], BF16)
-        nc.vector.memset(ones_bf[:], 1.0)
+            nc.scalar.dma_start(out=par_b[:, i, :], in_=vec.partition_broadcast(P))
 
         load_trig(0, CHUNK)
         load_x(0)
@@ -119,10 +116,6 @@ def tile_groupqueryattention_pa_t_kernel(
         nc.vector.memset(eps_col[:], EPS)
         warm = const.tile([P, 1], F32)
         nc.scalar.activation(out=warm[:], in_=eps_col[:], func=ACT.Abs_reciprocal_sqrt)
-        par_ps = psum.tile([P, 4 * DH], F32, tag="shift", bufs=1, name="par_ps")
-        nc.tensor.matmul(out=par_ps[:], lhsT=ones_bf[:], rhs=par_rows[:], start=True, stop=True)
-        par_b = const.tile([P, 4, DH], BF16)
-        nc.vector.tensor_copy(out=par_b[:].rearrange("p i d -> p (i d)"), in_=par_ps[:])
 
         def rot(out, in_):
             nc.vector.tensor_scalar_mul(out=out[:, :, 0:HALF], in0=in_[:, :, HALF:DH], scalar1=-1.0)
@@ -206,7 +199,7 @@ def tile_groupqueryattention_pa_t_kernel(
                 banks.append(ub)
             return banks
 
-        def rotate(t, banks, adder):
+        def rotate(t, banks, pieces):
             prod = work.tile([P, 2, BLOCKS, DH], F32, name="prod")
             sumsq = work.tile([P, BLOCKS], F32, name="sumsq")
             for j in range(BLOCKS // BANK_BLOCKS):
@@ -226,10 +219,11 @@ def tile_groupqueryattention_pa_t_kernel(
                     )
             w1 = prod[:, 0, :, :]
             halves = "p n (h d) -> p n h d"
-            adder.tensor_tensor(
-                out=w1.rearrange(halves, h=2), in0=w1.rearrange(halves, h=2),
-                in1=prod[:, 1, :, :].rearrange(halves, h=2)[:, :, ::-1, :], op=ALU.add,
-            )
+            for n0, n1 in pieces:
+                nc.gpsimd.tensor_tensor(
+                    out=prod[:, 0, n0:n1, :].rearrange(halves, h=2), in0=prod[:, 0, n0:n1, :].rearrange(halves, h=2),
+                    in1=prod[:, 1, n0:n1, :].rearrange(halves, h=2)[:, :, ::-1, :], op=ALU.add,
+                )
             rstd = work.tile([P, BLOCKS], F32, name="rstd")
             nc.scalar.activation(
                 out=rstd[:], in_=sumsq[:], func=ACT.Abs_reciprocal_sqrt, bias=eps_col[:, 0:1], scale=1.0 / DH
@@ -277,7 +271,7 @@ def tile_groupqueryattention_pa_t_kernel(
 
         def finish(t, w1, rstd, shift_q):
             rk = stage.tile([P, B, DH], F32, name="rk")
-            on_vector = K_ON_VECTOR if t < T - 1 else B
+            on_vector = K_ON_VECTOR if t < T - 2 else B
             for b in range(on_vector):
                 nc.vector.scalar_tensor_tensor(
                     out=rk[:, b, :], in0=w1[:, b, :], scalar=rstd[:, b : b + 1],
@@ -308,7 +302,6 @@ def tile_groupqueryattention_pa_t_kernel(
         build_tables(nc.vector, CHUNK)
         build_tables(nc.gpsimd, 2 * CHUNK)
         build_tables(nc.gpsimd, 3 * CHUNK)
-        grouped_of[1] = group_x(transpose_x(1))
         transpose_trig(0)
         banks_of = {0: project(mx_of[0])}
         rot(shift_rot, par_b[:, 2:4, :])
@@ -316,7 +309,7 @@ def tile_groupqueryattention_pa_t_kernel(
         nc.vector.tensor_tensor(out=diag_shift[:], in0=ident_pair, in1=par_b[:, 2:4, :], op=ALU.mult)
         nc.vector.tensor_tensor(out=diag_shift_rot[:], in0=ident_pair, in1=shift_rot[:], op=ALU.mult)
         rotate_shift_k(0)
-        mx_of[1] = quantise(grouped_of[1])
+        grouped_of[1] = group_x(transpose_x(1))
         grouped_of[2] = group_x(transpose_x(2))
 
         done_of = {}
@@ -325,9 +318,12 @@ def tile_groupqueryattention_pa_t_kernel(
             if n + 3 < T:
                 xt_banks = transpose_x(n + 3)
             if n < T:
-                done_of[n] = rotate(n, banks_of[n], nc.gpsimd if n < T - 1 else nc.vector)
+                last = ((0, 2 * BANK_BLOCKS), (2 * BANK_BLOCKS, BLOCKS))
+                done_of[n] = rotate(n, banks_of[n], ((0, BLOCKS),) if n < T - 1 else last)
             if n + 3 < T:
                 grouped_of[n + 3] = group_x(xt_banks)
+            if n == 0:
+                mx_of[1] = quantise(grouped_of[1])
             if n + 2 < T:
                 mx_of[n + 2] = quantise(grouped_of[n + 2])
             if n >= 1:

@@ -22,10 +22,10 @@ HALF = DH // 2
 EPS = 1e-6
 T = S // P
 N_ALL = (H + 2) * DH
-BLOCKS = B * (H + 1)
-BANK_BLOCKS = 4
+K_COL = H * DH
+V_COL = (H + 1) * DH
+QB = B * H
 CHUNK = 4
-K_ON_VECTOR = 1
 
 FLOPS = 2 * B * S * D * N_ALL
 
@@ -64,7 +64,7 @@ def tile_groupqueryattention_pa_t_kernel(
         quant = ctx.enter_context(tc.tile_pool(name="quant", bufs=2))
         work = ctx.enter_context(tc.tile_pool(name="work", bufs=3))
         stage = ctx.enter_context(tc.tile_pool(name="stage", bufs=4))
-        psum = ctx.enter_context(tc.psum_pool(name="psum", bufs=2))
+        psum = ctx.enter_context(tc.psum_pool(name="psum", bufs=1))
 
         x_tiles = []
         for t in range(T):
@@ -74,12 +74,18 @@ def tile_groupqueryattention_pa_t_kernel(
         def load_x(t):
             nc.sync.dma_start(out=x_tiles[t][:], in_=x_view[:, :, t, :])
 
-        cos_sb = const.tile([P, T, DH], BF16)
+        trig = const.tile([P, T, 2, DH], BF16)
         sin_sb = const.tile([P, T, DH], BF16)
 
         def load_trig(t0, t1):
-            nc.sync.dma_start(out=cos_sb[:, t0:t1, :], in_=cos_view[:, t0:t1, :])
+            nc.sync.dma_start(out=trig[:, t0:t1, 0, :], in_=cos_view[:, t0:t1, :])
             nc.sync.dma_start(out=sin_sb[:, t0:t1, :], in_=sin_view[:, t0:t1, :])
+
+        def swap_sin(engine, t0, t1):
+            engine.tensor_copy(out=trig[:, t0:t1, 1, 0:HALF], in_=sin_sb[:, t0:t1, HALF:DH])
+            engine.tensor_scalar(
+                out=trig[:, t0:t1, 1, HALF:DH], in0=sin_sb[:, t0:t1, 0:HALF], scalar1=-1.0, scalar2=None, op0=ALU.mult
+            )
 
         par_b = const.tile([P, 4, DH], BF16)
         for i, vec in enumerate((q_scale, k_scale, q_shift, k_shift)):
@@ -104,8 +110,7 @@ def tile_groupqueryattention_pa_t_kernel(
                     in_=scales[0, 4 * quad : 4 * quad + 4, :].bitcast(I32),
                 )
             col += n
-        load_x(1)
-        for t in range(2, T):
+        for t in range(1, T):
             load_x(t)
 
         ident_f32 = const.tile([P, P], F32)
@@ -117,37 +122,32 @@ def tile_groupqueryattention_pa_t_kernel(
         warm = const.tile([P, 1], F32)
         nc.scalar.activation(out=warm[:], in_=eps_col[:], func=ACT.Abs_reciprocal_sqrt)
 
-        def rot(out, in_):
-            nc.vector.tensor_scalar_mul(out=out[:, :, 0:HALF], in0=in_[:, :, HALF:DH], scalar1=-1.0)
-            nc.vector.tensor_copy(out=out[:, :, HALF:DH], in_=in_[:, :, 0:HALF])
+        def swap_columns(out, in_):
+            nc.gpsimd.tensor_copy(out=out[:, 0:HALF], in_=in_[:, HALF:DH])
+            nc.gpsimd.tensor_copy(out=out[:, HALF:DH], in_=in_[:, 0:HALF])
+
+        swap_f32 = const.tile([P, P], F32)
+        swap_columns(swap_f32, ident_f32)
+        swap_bf = const.tile([P, P], BF16)
+        swap_columns(swap_bf, ident_bf)
 
         gain = const.tile([P, 2, DH], F32)
         nc.vector.tensor_scalar_add(out=gain[:], in0=par_b[:, 0:2, :], scalar1=1.0)
-        gain_sign = const.tile([P, 2, DH], F32)
-        nc.vector.tensor_copy(out=gain_sign[:, :, 0:HALF], in_=gain[:, :, 0:HALF])
-        nc.vector.tensor_scalar_mul(out=gain_sign[:, :, HALF:DH], in0=gain[:, :, HALF:DH], scalar1=-1.0)
 
-        tab = const.tile([P, T, 2, 2, DH], F32)
+        tab = const.tile([P, T, 2, DH], F32)
 
-        def build_tables(engine, t0):
+        def build_table(engine, t0):
             engine.tensor_tensor(
-                out=tab[:, t0 : t0 + CHUNK, :, 0, :],
-                in0=cos_sb[:, t0 : t0 + CHUNK, :].unsqueeze(2).to_broadcast([P, CHUNK, 2, DH]),
-                in1=gain[:].unsqueeze(1).to_broadcast([P, CHUNK, 2, DH]),
+                out=tab[:, t0 : t0 + CHUNK, :, :],
+                in0=trig[:, t0 : t0 + CHUNK, :, :],
+                in1=gain[:, 0, :].unsqueeze(1).unsqueeze(1).to_broadcast([P, CHUNK, 2, DH]),
                 op=ALU.mult,
             )
-            for lo, other in ((0, HALF), (HALF, 0)):
-                engine.tensor_tensor(
-                    out=tab[:, t0 : t0 + CHUNK, :, 1, lo : lo + HALF],
-                    in0=sin_sb[:, t0 : t0 + CHUNK, other : other + HALF].unsqueeze(2).to_broadcast([P, CHUNK, 2, HALF]),
-                    in1=gain_sign[:, :, lo : lo + HALF].unsqueeze(1).to_broadcast([P, CHUNK, 2, HALF]),
-                    op=ALU.mult,
-                )
 
         def transpose_x(t):
             banks = []
             for j in range(B // 2):
-                xt = psum.tile([P, 2, 2, P], F32, tag="xt", name="xt")
+                xt = psum.tile([P, 2, 2, P], F32, tag="xt", bufs=2, name="xt")
                 for i in range(2):
                     x_words = x_tiles[t][:, 2 * j + i, :].bitcast(F32)
                     for u in range(2):
@@ -155,14 +155,14 @@ def tile_groupqueryattention_pa_t_kernel(
                 banks.append(xt)
             return banks
 
-        def group_x(banks):
-            grouped = quant.tile([P, B, P, 2], F32, align_bytes=64, name="grouped")
-            for j in range(B // 2):
-                nc.scalar.copy(
-                    out=grouped[:, 2 * j : 2 * j + 2, :, :],
-                    in_=banks[j][:].rearrange("p i u r -> p i r u"),
-                )
-            return grouped
+        def new_group():
+            return quant.tile([P, B, P, 2], F32, align_bytes=64, name="grouped")
+
+        def group_x(grouped, banks, j):
+            nc.scalar.copy(
+                out=grouped[:, 2 * j : 2 * j + 2, :, :],
+                in_=banks[j][:].rearrange("p i u r -> p i r u"),
+            )
 
         def quantise(grouped):
             codes = quant.tile([P, B * P], U32, align_bytes=64, bufs=3, name="codes")
@@ -186,152 +186,212 @@ def tile_groupqueryattention_pa_t_kernel(
             )
 
         def project(mx):
-            banks = []
-            for j in range(4):
-                ub = psum.tile([P, BANK_BLOCKS * DH], F32, tag="ubank", bufs=5, name="ub")
-                if j == 1 or j == 2:
+            kt = psum.tile([P, B, P], F32, tag="kt", name="kt")
+            nc.tensor.matmul_mx(
+                out=kt[:].rearrange("p b r -> p (b r)"),
+                lhsT=w_codes[:, 4 * K_COL : 4 * V_COL].bitcast(FP8X4),
+                lhsT_scale=w_scales[:, K_COL:V_COL],
+                rhs=mx[0][:].bitcast(FP8X4),
+                rhs_scale=mx[1][:],
+                start=True,
+                stop=True,
+            )
+            banks = {}
+            for kind, c0 in (("kv", K_COL), ("q", 0)):
+                for j in range(2):
+                    bank = psum.tile([P, 2, 2, DH], F32, tag="%s%d" % (kind, j), name=kind)
                     for i in range(2):
-                        pass_x(ub[:, i * H * DH : (i + 1) * H * DH], mx, 2 * (j - 1) + i, 0, H * DH)
-                else:
-                    c0 = H * DH if j == 0 else (H + 1) * DH
-                    for b in range(B):
-                        pass_x(ub[:, b * DH : (b + 1) * DH], mx, b, c0, c0 + DH)
-                banks.append(ub)
-            return banks
+                        pass_x(bank[:, i, :, :].rearrange("p c d -> p (c d)"), mx, 2 * j + i, c0, c0 + 2 * DH)
+                    banks[kind, j] = bank
+            return kt, banks
 
-        def rotate(t, banks, pieces):
-            prod = work.tile([P, 2, BLOCKS, DH], F32, name="prod")
-            sumsq = work.tile([P, BLOCKS], F32, name="sumsq")
-            for j in range(BLOCKS // BANK_BLOCKS):
-                c = 1 if j == 0 else 0
+        shift_swap = const.tile([P, 2, DH], BF16)
+        diag_shift = const.tile([P, 2, DH], BF16)
+        diag_shift_swap = const.tile([P, 2, DH], BF16)
+        trig_t = const.tile([P, T, 2, P], BF16)
+        shift_k = const.tile([P, T, DH], F32)
+        gain_k = const.tile([P, 1], F32)
+
+        def rotate_shift(out, t, c):
+            nc.tensor.matmul(out=out, lhsT=trig_t[:, t, 0, :], rhs=diag_shift[:, c, :], start=True, stop=False)
+            nc.tensor.matmul(out=out, lhsT=trig_t[:, t, 1, :], rhs=diag_shift_swap[:, c, :], start=False, stop=True)
+
+        def transpose_trig(t0):
+            tp = psum.tile([P, CHUNK, 2, P], BF16, tag="xt", bufs=2, name="tp")
+            for j in range(CHUNK):
+                for c in range(2):
+                    nc.tensor.transpose(tp[:, j, c, :], trig[:, t0 + j, c, :], ident_bf[:])
+            nc.scalar.copy(out=trig_t[:, t0 : t0 + CHUNK, :, :], in_=tp[:])
+
+        def rotate_shift_k(t0):
+            sk = psum.tile([P, CHUNK, DH], F32, tag="xt", bufs=2, name="sk")
+            for j in range(CHUNK):
+                rotate_shift(sk[:, j, :], t0 + j, 1)
+            nc.scalar.copy(out=shift_k[:, t0 : t0 + CHUNK, :], in_=sk[:])
+
+        def rotate_shift_q(t):
+            shift_q = psum.tile([P, DH], F32, tag="shift", name="shift_q")
+            rotate_shift(shift_q[:], t, 0)
+            return shift_q
+
+        def squares(blocks, name):
+            n = len(blocks)
+            sumsq = work.tile([P, n], F32, name="sumsq_" + name)
+            for i, blk in enumerate(blocks):
+                junk = work.tile([P, DH], F32, name="junk")
+                nc.scalar.activation(out=junk[:], in_=blk, func=ACT.Square, accum_out=sumsq[:, i : i + 1])
+            rstd = work.tile([P, n], F32, name="rstd_" + name)
+            nc.scalar.activation(
+                out=rstd[:], in_=sumsq[:], func=ACT.Abs_reciprocal_sqrt, bias=eps_col[:, 0:1], scale=1.0 / DH
+            )
+            return rstd
+
+        def multiply_k(t, kt):
+            prod_k = work.tile([P, 2, B, P], F32, name="prod_k")
+            for c in range(2):
+                nc.vector.scalar_tensor_tensor(
+                    out=prod_k[:, c, :, :],
+                    in0=kt[:],
+                    scalar=gain_k[:, 0:1],
+                    in1=trig_t[:, t, c, :].unsqueeze(1).to_broadcast([P, B, P]),
+                    op0=ALU.mult,
+                    op1=ALU.mult,
+                )
+            return prod_k
+
+        def add_k(prod_k):
+            wk = psum.tile([P, B, P], F32, tag="kt", name="wk")
+            for b in range(B):
+                for c, perm in enumerate((ident_f32, swap_f32)):
+                    nc.tensor.matmul(
+                        out=wk[:, b, :], lhsT=prod_k[:, c, b, :], rhs=perm[:], is_transpose=True,
+                        start=(c == 0), stop=(c == 1),
+                    )
+            return wk
+
+        def multiply_q(t, banks, prod):
+            for j in range(2):
                 nc.vector.tensor_tensor(
-                    out=prod[:, :, BANK_BLOCKS * j : BANK_BLOCKS * (j + 1), :],
-                    in0=banks[j][:].rearrange("p (n d) -> p n d", d=DH).unsqueeze(1).to_broadcast([P, 2, BANK_BLOCKS, DH]),
-                    in1=tab[:, t, c, :, :].unsqueeze(2).to_broadcast([P, 2, BANK_BLOCKS, DH]),
+                    out=prod[:, :, 4 * j : 4 * j + 4, :],
+                    in0=banks["q", j][:].rearrange("p i h d -> p (i h) d").unsqueeze(1).to_broadcast([P, 2, 4, DH]),
+                    in1=tab[:, t, :, :].unsqueeze(2).to_broadcast([P, 2, 4, DH]),
                     op=ALU.mult,
                 )
-                for i in range(BANK_BLOCKS):
-                    blk = BANK_BLOCKS * j + i
-                    junk = work.tile([P, DH], F32, name="junk")
-                    nc.scalar.activation(
-                        out=junk[:], in_=banks[j][:, i * DH : (i + 1) * DH], func=ACT.Square,
-                        accum_out=sumsq[:, blk : blk + 1],
-                    )
-            w1 = prod[:, 0, :, :]
+
+        def add_q(prod, pieces):
             halves = "p n (h d) -> p n h d"
             for n0, n1 in pieces:
                 nc.gpsimd.tensor_tensor(
                     out=prod[:, 0, n0:n1, :].rearrange(halves, h=2), in0=prod[:, 0, n0:n1, :].rearrange(halves, h=2),
                     in1=prod[:, 1, n0:n1, :].rearrange(halves, h=2)[:, :, ::-1, :], op=ALU.add,
                 )
-            rstd = work.tile([P, BLOCKS], F32, name="rstd")
-            nc.scalar.activation(
-                out=rstd[:], in_=sumsq[:], func=ACT.Abs_reciprocal_sqrt, bias=eps_col[:, 0:1], scale=1.0 / DH
-            )
+
+        def store_v(t, banks):
             rv = stage.tile([P, B, DH], F32, name="rv")
-            nc.scalar.copy(out=rv[:].rearrange("p b d -> p (b d)"), in_=banks[3][:])
+            for j in range(2):
+                nc.scalar.copy(out=rv[:, 2 * j : 2 * j + 2, :], in_=banks["kv", j][:, :, 1, :])
             nc.sync.dma_start(out=v_view[:, :, t, :], in_=rv[:])
-            return w1, rstd
 
-        shift_rot = const.tile([P, 2, DH], BF16)
-        diag_shift = const.tile([P, 2, DH], BF16)
-        diag_shift_rot = const.tile([P, 2, DH], BF16)
-        trig_t = const.tile([P, T, 2, P], BF16)
-        shift_k = const.tile([P, T, DH], F32)
+        def scale_k(wk, rstd_k):
+            zk = work.tile([P, B, DH], F32, name="zk")
+            for b in range(B):
+                nc.scalar.activation(out=zk[:, b, :], in_=wk[:, b, :], func=ACT.Copy, scale=rstd_k[:, b : b + 1])
+            return zk
 
-        def rotate_shift(out, t, c):
-            nc.tensor.matmul(out=out, lhsT=trig_t[:, t, 0, :], rhs=diag_shift[:, c, :], start=True, stop=False)
-            nc.tensor.matmul(out=out, lhsT=trig_t[:, t, 1, :], rhs=diag_shift_rot[:, c, :], start=False, stop=True)
-
-        def transpose_trig(t0):
-            tp = psum.tile([P, CHUNK, 2, P], BF16, tag="xt", name="tp")
-            for j in range(CHUNK):
-                nc.tensor.transpose(tp[:, j, 0, :], cos_sb[:, t0 + j, :], ident_bf[:])
-                nc.tensor.transpose(tp[:, j, 1, :], sin_sb[:, t0 + j, :], ident_bf[:])
-            nc.scalar.copy(out=trig_t[:, t0 : t0 + CHUNK, :, :], in_=tp[:])
-
-        def rotate_shift_k(t0):
-            sk = psum.tile([P, CHUNK, DH], F32, tag="xt", name="sk")
-            for j in range(CHUNK):
-                rotate_shift(sk[:, j, :], t0 + j, 1)
-            nc.scalar.copy(out=shift_k[:, t0 : t0 + CHUNK, :], in_=sk[:])
-
-        def rotate_shift_q(t):
-            shift_q = psum.tile([P, 2, DH], F32, tag="shift", bufs=1, name="shift_q")
-            both = "p c d -> p (c d)"
-            nc.tensor.matmul(
-                out=shift_q[:].rearrange(both), lhsT=trig_t[:, t, 0, :], rhs=diag_shift[:].rearrange(both),
-                start=True, stop=False,
-            )
-            nc.tensor.matmul(
-                out=shift_q[:].rearrange(both), lhsT=trig_t[:, t, 1, :], rhs=diag_shift_rot[:].rearrange(both),
-                start=False, stop=True,
-            )
-            return shift_q
-
-        def finish(t, w1, rstd, shift_q):
+        def shift_k_on_gpsimd(t, zk):
             rk = stage.tile([P, B, DH], F32, name="rk")
-            on_vector = K_ON_VECTOR if t < T - 2 else B
-            for b in range(on_vector):
+            nc.gpsimd.tensor_tensor(
+                out=rk[:], in0=zk[:], in1=shift_k[:, t, :].unsqueeze(1).to_broadcast([P, B, DH]), op=ALU.add
+            )
+            return rk
+
+        def finish_k_on_vector(t, wk, rstd_k):
+            rk = stage.tile([P, B, DH], F32, name="rk")
+            for b in range(B):
                 nc.vector.scalar_tensor_tensor(
-                    out=rk[:, b, :], in0=w1[:, b, :], scalar=rstd[:, b : b + 1],
-                    in1=shift_q[:, 1, :], op0=ALU.mult, op1=ALU.add,
+                    out=rk[:, b, :], in0=wk[:, b, :], scalar=rstd_k[:, b : b + 1], in1=shift_k[:, t, :],
+                    op0=ALU.mult, op1=ALU.add,
                 )
-            if on_vector < B:
-                zk = work.tile([P, B, DH], F32, name="zk")
-                for b in range(on_vector, B):
-                    nc.scalar.activation(out=zk[:, b, :], in_=w1[:, b, :], func=ACT.Copy, scale=rstd[:, b : b + 1])
-                nc.gpsimd.tensor_tensor(
-                    out=rk[:, on_vector:B, :], in0=zk[:, on_vector:B, :],
-                    in1=shift_k[:, t, :].unsqueeze(1).to_broadcast([P, B - on_vector, DH]), op=ALU.add,
-                )
-            nc.sync.dma_start(out=k_view[:, :, t, :], in_=rk[:])
-            rq = stage.tile([P, B * H, DH], F32, name="rq")
-            step = B * H // 2 if t == T - 1 else B * H
-            for i in range(B * H):
+            return rk
+
+        def finish_q(t, prod, rstd_q, shift_q):
+            rq = stage.tile([P, QB, DH], F32, name="rq")
+            step = QB // 2 if t == T - 1 else QB
+            for i in range(QB):
                 nc.vector.scalar_tensor_tensor(
-                    out=rq[:, i, :], in0=w1[:, B + i, :], scalar=rstd[:, B + i : B + i + 1],
-                    in1=shift_q[:, 0, :], op0=ALU.mult, op1=ALU.add,
+                    out=rq[:, i, :], in0=prod[:, 0, i, :], scalar=rstd_q[:, i : i + 1],
+                    in1=shift_q[:], op0=ALU.mult, op1=ALU.add,
                 )
                 if (i + 1) % step == 0:
                     nc.sync.dma_start(out=q_view[:, i + 1 - step : i + 1, t, :], in_=rq[:, i + 1 - step : i + 1, :])
 
-        grouped_of = {0: group_x(transpose_x(0))}
-        build_tables(nc.vector, 0)
-        mx_of = {0: quantise(grouped_of[0])}
-        build_tables(nc.vector, CHUNK)
-        build_tables(nc.gpsimd, 2 * CHUNK)
-        build_tables(nc.gpsimd, 3 * CHUNK)
-        transpose_trig(0)
-        banks_of = {0: project(mx_of[0])}
-        rot(shift_rot, par_b[:, 2:4, :])
-        ident_pair = ident_bf[:].unsqueeze(1).to_broadcast([P, 2, P])
-        nc.vector.tensor_tensor(out=diag_shift[:], in0=ident_pair, in1=par_b[:, 2:4, :], op=ALU.mult)
-        nc.vector.tensor_tensor(out=diag_shift_rot[:], in0=ident_pair, in1=shift_rot[:], op=ALU.mult)
-        rotate_shift_k(0)
-        grouped_of[1] = group_x(transpose_x(1))
-        grouped_of[2] = group_x(transpose_x(2))
+        def start_group(t):
+            banks = transpose_x(t)
+            grouped = new_group()
+            for j in range(2):
+                group_x(grouped, banks, j)
+            return grouped
 
-        done_of = {}
-        shift_of = {}
+        grouped_of = {0: start_group(0)}
+        gt = psum.tile([P, P], F32, tag="shift", name="gt")
+        nc.tensor.transpose(gt[:], gain[:, 1, :], ident_f32[:])
+        nc.scalar.copy(out=gain_k[:], in_=gt[:, 0:1])
+        swap_sin(nc.vector, 0, CHUNK)
+        transpose_trig(0)
+        build_table(nc.vector, 0)
+        mx_of = {0: quantise(grouped_of[0])}
+        swap_sin(nc.vector, CHUNK, T)
+        for t0 in range(CHUNK, T, CHUNK):
+            build_table(nc.gpsimd, t0)
+        next_k, next_banks = project(mx_of[0])
+        nc.vector.tensor_copy(out=shift_swap[:, :, 0:HALF], in_=par_b[:, 2:4, HALF:DH])
+        nc.vector.tensor_copy(out=shift_swap[:, :, HALF:DH], in_=par_b[:, 2:4, 0:HALF])
+        for out, mat, vec in ((diag_shift, ident_bf, par_b[:, 2:4, :]), (diag_shift_swap, swap_bf, shift_swap[:])):
+            nc.vector.tensor_tensor(
+                out=out[:], in0=mat[:].unsqueeze(1).to_broadcast([P, 2, P]), in1=vec, op=ALU.mult
+            )
+        rotate_shift_k(0)
+        grouped_of[1] = start_group(1)
+        grouped_of[2] = start_group(2)
+
+        before = None
         for n in range(T + 1):
-            if n + 3 < T:
-                xt_banks = transpose_x(n + 3)
             if n < T:
-                last = ((0, 2 * BANK_BLOCKS), (2 * BANK_BLOCKS, BLOCKS))
-                done_of[n] = rotate(n, banks_of[n], ((0, BLOCKS),) if n < T - 1 else last)
-            if n + 3 < T:
-                grouped_of[n + 3] = group_x(xt_banks)
-            if n == 0:
-                mx_of[1] = quantise(grouped_of[1])
-            if n + 2 < T:
-                mx_of[n + 2] = quantise(grouped_of[n + 2])
+                kt, banks = next_k, next_banks
+                xt_banks = transpose_x(n + 3) if n + 3 < T else None
+                prod_k = multiply_k(n, kt)
+                wk = add_k(prod_k)
+                prod = work.tile([P, 2, QB, DH], F32, name="prod")
+                multiply_q(n, banks, prod)
+
+                rstd_k = squares([banks["kv", j][:, i, 0, :] for j in range(2) for i in range(2)], "k")
+                store_v(n, banks)
+                if xt_banks:
+                    grouped_of[n + 3] = new_group()
+                    group_x(grouped_of[n + 3], xt_banks, 0)
+                if n < T - 1:
+                    zk = scale_k(wk, rstd_k)
+                if xt_banks:
+                    group_x(grouped_of[n + 3], xt_banks, 1)
+                rstd_q = squares([banks["q", j][:, i, h, :] for j in range(2) for i in range(2) for h in range(H)], "q")
+
+                add_q(prod, ((0, QB),) if n < T - 1 else ((0, QB // 2), (QB // 2, QB)))
+                if n < T - 1:
+                    rk = shift_k_on_gpsimd(n, zk)
+                if n == 0:
+                    mx_of[1] = quantise(grouped_of[1])
+                if n + 2 < T:
+                    mx_of[n + 2] = quantise(grouped_of[n + 2])
+                if n == T - 1:
+                    rk = finish_k_on_vector(n, wk, rstd_k)
             if n >= 1:
-                finish(n - 1, done_of[n - 1][0], done_of[n - 1][1], shift_of[n - 1])
+                nc.sync.dma_start(out=k_view[:, :, n - 1, :], in_=before[3][:])
+                finish_q(n - 1, *before[:3])
             if n + 1 < T:
-                banks_of[n + 1] = project(mx_of[n + 1])
+                next_k, next_banks = project(mx_of[n + 1])
             if n < T:
-                shift_of[n] = rotate_shift_q(n)
+                shift_q = rotate_shift_q(n)
+                before = (prod, rstd_q, shift_q, rk)
             if n % CHUNK == 1 and n + CHUNK - 1 < T:
                 transpose_trig(n + CHUNK - 1)
             if n % CHUNK == 2 and n + CHUNK - 2 < T:

@@ -91,9 +91,8 @@ def tile_groupqueryattention_pa_t_kernel(
         for i, vec in enumerate((q_scale, k_scale, q_shift, k_shift)):
             nc.scalar.dma_start(out=par_b[:, i, :], in_=vec.partition_broadcast(P))
 
-        load_trig(0, CHUNK)
         load_x(0)
-        load_trig(CHUNK, T)
+        load_trig(0, CHUNK)
         w_codes = const.tile([P, 4 * N_ALL], U8, align_bytes=64)
         w_scales = const.tile([P, N_ALL], U8, align_bytes=64)
         nc.vector.memset(w_scales[:].bitcast(I32), 0)
@@ -110,7 +109,9 @@ def tile_groupqueryattention_pa_t_kernel(
                     in_=scales[0, 4 * quad : 4 * quad + 4, :].bitcast(I32),
                 )
             col += n
-        for t in range(1, T):
+        load_x(1)
+        load_trig(CHUNK, T)
+        for t in range(2, T):
             load_x(t)
 
         ident_f32 = const.tile([P, P], F32)
@@ -136,11 +137,11 @@ def tile_groupqueryattention_pa_t_kernel(
 
         tab = const.tile([P, T, 2, DH], F32)
 
-        def build_table(engine, t0):
+        def build_table(engine, t0, t1):
             engine.tensor_tensor(
-                out=tab[:, t0 : t0 + CHUNK, :, :],
-                in0=trig[:, t0 : t0 + CHUNK, :, :],
-                in1=gain[:, 0, :].unsqueeze(1).unsqueeze(1).to_broadcast([P, CHUNK, 2, DH]),
+                out=tab[:, t0:t1, :, :],
+                in0=trig[:, t0:t1, :, :],
+                in1=gain[:, 0, :].unsqueeze(1).unsqueeze(1).to_broadcast([P, t1 - t0, 2, DH]),
                 op=ALU.mult,
             )
 
@@ -158,8 +159,8 @@ def tile_groupqueryattention_pa_t_kernel(
         def new_group():
             return quant.tile([P, B, P, 2], F32, align_bytes=64, name="grouped")
 
-        def group_x(grouped, banks, j):
-            nc.scalar.copy(
+        def group_x(grouped, banks, j, copy=nc.scalar.copy):
+            copy(
                 out=grouped[:, 2 * j : 2 * j + 2, :, :],
                 in_=banks[j][:].rearrange("p i u r -> p i r u"),
             )
@@ -212,34 +213,39 @@ def tile_groupqueryattention_pa_t_kernel(
         shift_k = const.tile([P, T, DH], F32)
         gain_k = const.tile([P, 1], F32)
 
-        def rotate_shift(out, t, c):
-            nc.tensor.matmul(out=out, lhsT=trig_t[:, t, 0, :], rhs=diag_shift[:, c, :], start=True, stop=False)
-            nc.tensor.matmul(out=out, lhsT=trig_t[:, t, 1, :], rhs=diag_shift_swap[:, c, :], start=False, stop=True)
+        def transpose_trig(out, t):
+            for c in range(2):
+                nc.tensor.transpose(out[:, c, :], trig[:, t, c, :], ident_bf[:])
 
-        def transpose_trig(t0):
-            tp = psum.tile([P, CHUNK, 2, P], BF16, tag="xt", bufs=2, name="tp")
-            for j in range(CHUNK):
-                for c in range(2):
-                    nc.tensor.transpose(tp[:, j, c, :], trig[:, t0 + j, c, :], ident_bf[:])
-            nc.scalar.copy(out=trig_t[:, t0 : t0 + CHUNK, :, :], in_=tp[:])
+        def rotate_shifts(t, ahead):
+            tag, bufs = ("shift", 1) if t < T - 1 else ("xt", 2)
+            bank = psum.tile([P, 4, DH], F32, tag=tag, bufs=bufs, name="bank")
+            both = "p c d -> p (c d)"
+            for c, diag in enumerate((diag_shift, diag_shift_swap)):
+                nc.tensor.matmul(
+                    out=bank[:, 0:2, :].rearrange(both), lhsT=trig_t[:, t, c, :], rhs=diag[:].rearrange(both),
+                    start=(c == 0), stop=(c == 1),
+                )
+            if ahead < T:
+                transpose_trig(bank[:, 2, :].bitcast(BF16).rearrange("p (c r) -> p c r", c=2), ahead)
+            return bank
 
-        def rotate_shift_k(t0):
-            sk = psum.tile([P, CHUNK, DH], F32, tag="xt", bufs=2, name="sk")
-            for j in range(CHUNK):
-                rotate_shift(sk[:, j, :], t0 + j, 1)
-            nc.scalar.copy(out=shift_k[:, t0 : t0 + CHUNK, :], in_=sk[:])
-
-        def rotate_shift_q(t):
-            shift_q = psum.tile([P, DH], F32, tag="shift", name="shift_q")
-            rotate_shift(shift_q[:], t, 0)
-            return shift_q
+        def copy_shifts(t, bank, ahead):
+            if ahead < T:
+                nc.scalar.copy(
+                    out=trig_t[:, ahead, :, :],
+                    in_=bank[:, 2, :].bitcast(BF16).rearrange("p (c r) -> p c r", c=2),
+                )
+            nc.scalar.copy(out=shift_k[:, t, :], in_=bank[:, 1, :])
 
         def squares(blocks, name):
-            n = len(blocks)
-            sumsq = work.tile([P, n], F32, name="sumsq_" + name)
+            sumsq = work.tile([P, len(blocks)], F32, name="sumsq_" + name)
             for i, blk in enumerate(blocks):
                 junk = work.tile([P, DH], F32, name="junk")
                 nc.scalar.activation(out=junk[:], in_=blk, func=ACT.Square, accum_out=sumsq[:, i : i + 1])
+            return sumsq
+
+        def inverse_rms(sumsq, n, name):
             rstd = work.tile([P, n], F32, name="rstd_" + name)
             nc.scalar.activation(
                 out=rstd[:], in_=sumsq[:], func=ACT.Abs_reciprocal_sqrt, bias=eps_col[:, 0:1], scale=1.0 / DH
@@ -269,8 +275,10 @@ def tile_groupqueryattention_pa_t_kernel(
                     )
             return wk
 
-        def multiply_q(t, banks, prod):
+        def multiply_q(t, banks, prod, early):
             for j in range(2):
+                if j == 1 and early is not None:
+                    mx_of[early] = quantise(grouped_of[early])
                 nc.vector.tensor_tensor(
                     out=prod[:, :, 4 * j : 4 * j + 4, :],
                     in0=banks["q", j][:].rearrange("p i h d -> p (i h) d").unsqueeze(1).to_broadcast([P, 2, 4, DH]),
@@ -280,8 +288,8 @@ def tile_groupqueryattention_pa_t_kernel(
 
         def add_q(prod, pieces):
             halves = "p n (h d) -> p n h d"
-            for n0, n1 in pieces:
-                nc.gpsimd.tensor_tensor(
+            for engine, n0, n1 in pieces:
+                engine.tensor_tensor(
                     out=prod[:, 0, n0:n1, :].rearrange(halves, h=2), in0=prod[:, 0, n0:n1, :].rearrange(halves, h=2),
                     in1=prod[:, 1, n0:n1, :].rearrange(halves, h=2)[:, :, ::-1, :], op=ALU.add,
                 )
@@ -320,7 +328,7 @@ def tile_groupqueryattention_pa_t_kernel(
             for i in range(QB):
                 nc.vector.scalar_tensor_tensor(
                     out=rq[:, i, :], in0=prod[:, 0, i, :], scalar=rstd_q[:, i : i + 1],
-                    in1=shift_q[:], op0=ALU.mult, op1=ALU.add,
+                    in1=shift_q[:, 0, :], op0=ALU.mult, op1=ALU.add,
                 )
                 if (i + 1) % step == 0:
                     nc.sync.dma_start(out=q_view[:, i + 1 - step : i + 1, t, :], in_=rq[:, i + 1 - step : i + 1, :])
@@ -332,67 +340,87 @@ def tile_groupqueryattention_pa_t_kernel(
                 group_x(grouped, banks, j)
             return grouped
 
-        grouped_of = {0: start_group(0)}
+        x_banks = transpose_x(0)
+        grouped_of = {0: new_group()}
+        group_x(grouped_of[0], x_banks, 0)
+        group_x(grouped_of[0], x_banks, 1, nc.vector.tensor_copy)
+        swap_sin(nc.vector, 0, CHUNK)
+        mx_of = {0: quantise(grouped_of[0])}
         gt = psum.tile([P, P], F32, tag="shift", name="gt")
         nc.tensor.transpose(gt[:], gain[:, 1, :], ident_f32[:])
         nc.scalar.copy(out=gain_k[:], in_=gt[:, 0:1])
-        swap_sin(nc.vector, 0, CHUNK)
-        transpose_trig(0)
-        build_table(nc.vector, 0)
-        mx_of = {0: quantise(grouped_of[0])}
-        swap_sin(nc.vector, CHUNK, T)
-        for t0 in range(CHUNK, T, CHUNK):
-            build_table(nc.gpsimd, t0)
+        tp = psum.tile([P, CHUNK, 2, P], BF16, tag="xt", bufs=2, name="tp")
+        for t in range(CHUNK):
+            transpose_trig(tp[:, t, :, :], t)
+        nc.scalar.copy(out=trig_t[:, 0:CHUNK, :, :], in_=tp[:])
+        build_table(nc.vector, 0, 2)
         next_k, next_banks = project(mx_of[0])
+        build_table(nc.gpsimd, 2, CHUNK)
         nc.vector.tensor_copy(out=shift_swap[:, :, 0:HALF], in_=par_b[:, 2:4, HALF:DH])
         nc.vector.tensor_copy(out=shift_swap[:, :, HALF:DH], in_=par_b[:, 2:4, 0:HALF])
         for out, mat, vec in ((diag_shift, ident_bf, par_b[:, 2:4, :]), (diag_shift_swap, swap_bf, shift_swap[:])):
             nc.vector.tensor_tensor(
                 out=out[:], in0=mat[:].unsqueeze(1).to_broadcast([P, 2, P]), in1=vec, op=ALU.mult
             )
-        rotate_shift_k(0)
-        grouped_of[1] = start_group(1)
-        grouped_of[2] = start_group(2)
 
         before = None
+        to_group = {0: (1, 2), 1: (3, 4)}
+        to_quantise = {0: (1,), 1: (2,)}
         for n in range(T + 1):
+            groups = [t for t in to_group.get(n, (n + 3,)) if t < T]
+            xt_banks = {}
             if n < T:
                 kt, banks = next_k, next_banks
-                xt_banks = transpose_x(n + 3) if n + 3 < T else None
                 prod_k = multiply_k(n, kt)
+                for t in groups[:1]:
+                    xt_banks[t] = transpose_x(t)
                 wk = add_k(prod_k)
                 prod = work.tile([P, 2, QB, DH], F32, name="prod")
-                multiply_q(n, banks, prod)
+                multiply_q(n, banks, prod, 3 if n == 2 else None)
+                if n == T - 1:
+                    shift = rotate_shifts(n, T)
 
-                rstd_k = squares([banks["kv", j][:, i, 0, :] for j in range(2) for i in range(2)], "k")
+                sumsq_k = squares([banks["kv", j][:, i, 0, :] for j in range(2) for i in range(2)], "k")
                 store_v(n, banks)
-                if xt_banks:
-                    grouped_of[n + 3] = new_group()
-                    group_x(grouped_of[n + 3], xt_banks, 0)
+                rstd_k = inverse_rms(sumsq_k, B, "k")
+                if n >= 1:
+                    copy_shifts(n - 1, before[2], n - 1 + CHUNK)
+                for t in groups[:1]:
+                    grouped_of[t] = new_group()
+                    group_x(grouped_of[t], xt_banks[t], 0)
+                if n == 0:
+                    group_x(grouped_of[1], xt_banks[1], 1)
                 if n < T - 1:
                     zk = scale_k(wk, rstd_k)
-                if xt_banks:
-                    group_x(grouped_of[n + 3], xt_banks, 1)
-                rstd_q = squares([banks["q", j][:, i, h, :] for j in range(2) for i in range(2) for h in range(H)], "q")
-
-                add_q(prod, ((0, QB),) if n < T - 1 else ((0, QB // 2), (QB // 2, QB)))
-                if n < T - 1:
-                    rk = shift_k_on_gpsimd(n, zk)
-                if n == 0:
-                    mx_of[1] = quantise(grouped_of[1])
-                if n + 2 < T:
-                    mx_of[n + 2] = quantise(grouped_of[n + 2])
+                for t in groups[1:]:
+                    grouped_of[t] = start_group(t)
+                sumsq_q = squares([banks["q", j][:, i, h, :] for j in range(2) for i in range(2) for h in range(H)], "q")
+                if n >= 1:
+                    for t in groups[:1]:
+                        group_x(grouped_of[t], xt_banks[t], 1)
+                rstd_q = inverse_rms(sumsq_q, QB, "q")
                 if n == T - 1:
-                    rk = finish_k_on_vector(n, wk, rstd_k)
+                    copy_shifts(n, shift, T)
+
+                if n >= 1:
+                    rk = shift_k_on_gpsimd(n - 1, before[3])
+                    nc.sync.dma_start(out=k_view[:, :, n - 1, :], in_=rk[:])
+                if n >= 1 and n + 3 < T:
+                    build_table(nc.gpsimd, n + 3, n + 4)
+                add_q(prod, ((nc.gpsimd, 0, QB),) if n < T - 1 else ((nc.gpsimd, 0, QB // 2), (nc.gpsimd, QB // 2, QB)))
+                for t in to_quantise.get(n, (n + 2,)):
+                    if t < T:
+                        mx_of[t] = quantise(grouped_of[t])
+            if n == 0:
+                swap_sin(nc.vector, CHUNK, T)
             if n >= 1:
-                nc.sync.dma_start(out=k_view[:, :, n - 1, :], in_=before[3][:])
-                finish_q(n - 1, *before[:3])
+                finish_q(n - 1, before[0], before[1], before[2])
+            if n == T - 1:
+                rk = finish_k_on_vector(n, wk, rstd_k)
+                nc.sync.dma_start(out=k_view[:, :, n, :], in_=rk[:])
             if n + 1 < T:
                 next_k, next_banks = project(mx_of[n + 1])
             if n < T:
-                shift_q = rotate_shift_q(n)
-                before = (prod, rstd_q, shift_q, rk)
-            if n % CHUNK == 1 and n + CHUNK - 1 < T:
-                transpose_trig(n + CHUNK - 1)
-            if n % CHUNK == 2 and n + CHUNK - 2 < T:
-                rotate_shift_k(n + CHUNK - 2)
+                if n < T - 1:
+                    shift = rotate_shifts(n, n + CHUNK)
+                before = (prod, rstd_q, shift, zk)

@@ -186,7 +186,7 @@ def tile_groupqueryattention_pa_t_kernel(
                 stop=True,
             )
 
-        def project(mx):
+        def project_kt(mx):
             kt = psum.tile([P, B, P], F32, tag="kt", name="kt")
             nc.tensor.matmul_mx(
                 out=kt[:].rearrange("p b r -> p (b r)"),
@@ -197,14 +197,16 @@ def tile_groupqueryattention_pa_t_kernel(
                 start=True,
                 stop=True,
             )
-            banks = {}
-            for kind, c0 in (("kv", K_COL), ("q", 0)):
-                for j in range(2):
-                    bank = psum.tile([P, 2, 2, DH], F32, tag="%s%d" % (kind, j), name=kind)
-                    for i in range(2):
-                        pass_x(bank[:, i, :, :].rearrange("p c d -> p (c d)"), mx, 2 * j + i, c0, c0 + 2 * DH)
-                    banks[kind, j] = bank
-            return kt, banks
+            return kt
+
+        def project(mx, kind, c0):
+            banks = []
+            for j in range(2):
+                bank = psum.tile([P, 2, 2, DH], F32, tag="%s%d" % (kind, j), name=kind)
+                for i in range(2):
+                    pass_x(bank[:, i, :, :].rearrange("p c d -> p (c d)"), mx, 2 * j + i, c0, c0 + 2 * DH)
+                banks.append(bank)
+            return banks
 
         shift_swap = const.tile([P, 2, DH], BF16)
         diag_shift = const.tile([P, 2, DH], BF16)
@@ -245,6 +247,15 @@ def tile_groupqueryattention_pa_t_kernel(
                 nc.scalar.activation(out=junk[:], in_=blk, func=ACT.Square, accum_out=sumsq[:, i : i + 1])
             return sumsq
 
+        def squares_q(sumsq, banks, j):
+            for i in range(2):
+                for h in range(H):
+                    junk = work.tile([P, DH], F32, name="junk")
+                    c = 4 * j + 2 * i + h
+                    nc.scalar.activation(
+                        out=junk[:], in_=banks[j][:, i, h, :], func=ACT.Square, accum_out=sumsq[:, c : c + 1]
+                    )
+
         def inverse_rms(sumsq, n, name):
             rstd = work.tile([P, n], F32, name="rstd_" + name)
             nc.scalar.activation(
@@ -275,16 +286,13 @@ def tile_groupqueryattention_pa_t_kernel(
                     )
             return wk
 
-        def multiply_q(t, banks, prod, early):
-            for j in range(2):
-                if j == 1 and early is not None:
-                    mx_of[early] = quantise(grouped_of[early])
-                nc.vector.tensor_tensor(
-                    out=prod[:, :, 4 * j : 4 * j + 4, :],
-                    in0=banks["q", j][:].rearrange("p i h d -> p (i h) d").unsqueeze(1).to_broadcast([P, 2, 4, DH]),
-                    in1=tab[:, t, :, :].unsqueeze(2).to_broadcast([P, 2, 4, DH]),
-                    op=ALU.mult,
-                )
+        def multiply_q(t, banks, prod, j):
+            nc.vector.tensor_tensor(
+                out=prod[:, :, 4 * j : 4 * j + 4, :],
+                in0=banks[j][:].rearrange("p i h d -> p (i h) d").unsqueeze(1).to_broadcast([P, 2, 4, DH]),
+                in1=tab[:, t, :, :].unsqueeze(2).to_broadcast([P, 2, 4, DH]),
+                op=ALU.mult,
+            )
 
         def add_q(prod, pieces):
             halves = "p n (h d) -> p n h d"
@@ -297,7 +305,7 @@ def tile_groupqueryattention_pa_t_kernel(
         def store_v(t, banks):
             rv = stage.tile([P, B, DH], F32, name="rv")
             for j in range(2):
-                nc.scalar.copy(out=rv[:, 2 * j : 2 * j + 2, :], in_=banks["kv", j][:, :, 1, :])
+                nc.scalar.copy(out=rv[:, 2 * j : 2 * j + 2, :], in_=banks[j][:, :, 1, :])
             nc.sync.dma_start(out=v_view[:, :, t, :], in_=rv[:])
 
         def scale_k(wk, rstd_k):
@@ -354,7 +362,9 @@ def tile_groupqueryattention_pa_t_kernel(
             transpose_trig(tp[:, t, :, :], t)
         nc.scalar.copy(out=trig_t[:, 0:CHUNK, :, :], in_=tp[:])
         build_table(nc.vector, 0, 2)
-        next_k, next_banks = project(mx_of[0])
+        kt_of = {0: project_kt(mx_of[0])}
+        q_of = {0: project(mx_of[0], "q", 0)}
+        kv_of = {0: project(mx_of[0], "kv", K_COL)}
         build_table(nc.gpsimd, 2, CHUNK)
         nc.vector.tensor_copy(out=shift_swap[:, :, 0:HALF], in_=par_b[:, 2:4, HALF:DH])
         nc.vector.tensor_copy(out=shift_swap[:, :, HALF:DH], in_=par_b[:, 2:4, 0:HALF])
@@ -364,40 +374,43 @@ def tile_groupqueryattention_pa_t_kernel(
             )
 
         before = None
-        to_group = {0: (1, 2), 1: (3, 4)}
-        to_quantise = {0: (1,), 1: (2,)}
+        xt_of = {1: transpose_x(1)}
         for n in range(T + 1):
-            groups = [t for t in to_group.get(n, (n + 3,)) if t < T]
-            xt_banks = {}
             if n < T:
-                kt, banks = next_k, next_banks
+                kt, q, kv = kt_of[n], q_of[n], kv_of[n]
                 prod_k = multiply_k(n, kt)
-                for t in groups[:1]:
-                    xt_banks[t] = transpose_x(t)
                 wk = add_k(prod_k)
+                if n + 2 < T:
+                    xt_of[n + 2] = transpose_x(n + 2)
                 prod = work.tile([P, 2, QB, DH], F32, name="prod")
-                multiply_q(n, banks, prod, 3 if n == 2 else None)
+                multiply_q(n, q, prod, 0)
+                sumsq_k = squares([kv[j][:, i, 0, :] for j in range(2) for i in range(2)], "k")
+                store_v(n, kv)
+                rstd_k = inverse_rms(sumsq_k, B, "k")
+                if n == 0:
+                    grouped_of[1] = new_group()
+                    for j in range(2):
+                        group_x(grouped_of[1], xt_of[1], j)
+                if n >= 1:
+                    copy_shifts(n - 1, before[2], n - 1 + CHUNK)
+                    if n + 1 < T:
+                        mx_of[n + 1] = quantise(grouped_of[n + 1])
+                if n < T - 1:
+                    zk = scale_k(wk, rstd_k)
+                multiply_q(n, q, prod, 1)
+                if n == 0:
+                    mx_of[1] = quantise(grouped_of[1])
+                    swap_sin(nc.vector, CHUNK, T)
                 if n == T - 1:
                     shift = rotate_shifts(n, T)
 
-                sumsq_k = squares([banks["kv", j][:, i, 0, :] for j in range(2) for i in range(2)], "k")
-                store_v(n, banks)
-                rstd_k = inverse_rms(sumsq_k, B, "k")
-                if n >= 1:
-                    copy_shifts(n - 1, before[2], n - 1 + CHUNK)
-                for t in groups[:1]:
-                    grouped_of[t] = new_group()
-                    group_x(grouped_of[t], xt_banks[t], 0)
-                if n == 0:
-                    group_x(grouped_of[1], xt_banks[1], 1)
-                if n < T - 1:
-                    zk = scale_k(wk, rstd_k)
-                for t in groups[1:]:
-                    grouped_of[t] = start_group(t)
-                sumsq_q = squares([banks["q", j][:, i, h, :] for j in range(2) for i in range(2) for h in range(H)], "q")
-                if n >= 1:
-                    for t in groups[:1]:
-                        group_x(grouped_of[t], xt_banks[t], 1)
+                sumsq_q = work.tile([P, QB], F32, name="sumsq_q")
+                if n + 2 < T:
+                    grouped_of[n + 2] = new_group()
+                for j in range(2):
+                    squares_q(sumsq_q, q, j)
+                    if n + 2 < T:
+                        group_x(grouped_of[n + 2], xt_of[n + 2], j)
                 rstd_q = inverse_rms(sumsq_q, QB, "q")
                 if n == T - 1:
                     copy_shifts(n, shift, T)
@@ -407,19 +420,16 @@ def tile_groupqueryattention_pa_t_kernel(
                     nc.sync.dma_start(out=k_view[:, :, n - 1, :], in_=rk[:])
                 if n >= 1 and n + 3 < T:
                     build_table(nc.gpsimd, n + 3, n + 4)
-                add_q(prod, ((nc.gpsimd, 0, QB),) if n < T - 1 else ((nc.gpsimd, 0, QB // 2), (nc.gpsimd, QB // 2, QB)))
-                for t in to_quantise.get(n, (n + 2,)):
-                    if t < T:
-                        mx_of[t] = quantise(grouped_of[t])
-            if n == 0:
-                swap_sin(nc.vector, CHUNK, T)
+                add_q(prod, ((nc.gpsimd, 0, QB // 2), (nc.gpsimd, QB // 2, QB)))
             if n >= 1:
                 finish_q(n - 1, before[0], before[1], before[2])
             if n == T - 1:
                 rk = finish_k_on_vector(n, wk, rstd_k)
                 nc.sync.dma_start(out=k_view[:, :, n, :], in_=rk[:])
             if n + 1 < T:
-                next_k, next_banks = project(mx_of[n + 1])
+                kt_of[n + 1] = project_kt(mx_of[n + 1])
+                kv_of[n + 1] = project(mx_of[n + 1], "kv", K_COL)
+                q_of[n + 1] = project(mx_of[n + 1], "q", 0)
             if n < T:
                 if n < T - 1:
                     shift = rotate_shifts(n, n + CHUNK)

@@ -63,7 +63,7 @@ def tile_groupqueryattention_pa_t_kernel(
         xpool = ctx.enter_context(tc.tile_pool(name="xpool", bufs=1))
         quant = ctx.enter_context(tc.tile_pool(name="quant", bufs=2))
         work = ctx.enter_context(tc.tile_pool(name="work", bufs=3))
-        stage = ctx.enter_context(tc.tile_pool(name="stage", bufs=4))
+        stage = ctx.enter_context(tc.tile_pool(name="stage", bufs=3))
         psum = ctx.enter_context(tc.psum_pool(name="psum", bufs=1))
 
         x_tiles = []
@@ -91,13 +91,11 @@ def tile_groupqueryattention_pa_t_kernel(
         for i, vec in enumerate((q_scale, k_scale, q_shift, k_shift)):
             nc.scalar.dma_start(out=par_b[:, i, :], in_=vec.partition_broadcast(P))
 
-        load_x(0)
-        load_trig(0, CHUNK)
         w_codes = const.tile([P, 4 * N_ALL], U8, align_bytes=64)
         w_scales = const.tile([P, N_ALL], U8, align_bytes=64)
         nc.vector.memset(w_scales[:].bitcast(I32), 0)
-        col = 0
-        for words, scales in ((wq_words, wq_scales), (wk_words, wk_scales), (wv_words, wv_scales)):
+
+        def load_w(words, scales, col):
             n = words.shape[2]
             nc.sync.dma_start(
                 out=w_codes[:, 4 * col : 4 * (col + n)].bitcast(I32),
@@ -108,10 +106,16 @@ def tile_groupqueryattention_pa_t_kernel(
                     out=w_scales[32 * quad : 32 * quad + 4, col : col + n].bitcast(I32),
                     in_=scales[0, 4 * quad : 4 * quad + 4, :].bitcast(I32),
                 )
-            col += n
+
+        load_x(0)
+        load_trig(0, CHUNK)
+        load_w(wk_words, wk_scales, K_COL)
+        load_w(wq_words, wq_scales, 0)
         load_x(1)
+        load_w(wv_words, wv_scales, V_COL)
+        load_x(2)
         load_trig(CHUNK, T)
-        for t in range(2, T):
+        for t in range(3, T):
             load_x(t)
 
         ident_f32 = const.tile([P, P], F32)
@@ -302,11 +306,24 @@ def tile_groupqueryattention_pa_t_kernel(
                     in1=prod[:, 1, n0:n1, :].rearrange(halves, h=2)[:, :, ::-1, :], op=ALU.add,
                 )
 
+        staged = {}
+
+        def stage_for(name, t, blocks):
+            if t % 2 == 0 or t == T - 1:
+                staged[name] = stage.tile([P, blocks, 2, DH], F32, name=name)
+            return staged[name][:, :, t % 2, :]
+
+        def store(name, view, t):
+            if t >= T - 2:
+                nc.sync.dma_start(out=view[:, :, t, :], in_=staged[name][:, :, t % 2, :])
+            elif t % 2 == 1:
+                nc.sync.dma_start(out=view[:, :, t - 1 : t + 1, :], in_=staged[name][:])
+
         def store_v(t, banks):
-            rv = stage.tile([P, B, DH], F32, name="rv")
+            rv = stage_for("rv", t, B)
             for j in range(2):
                 nc.scalar.copy(out=rv[:, 2 * j : 2 * j + 2, :], in_=banks[j][:, :, 1, :])
-            nc.sync.dma_start(out=v_view[:, :, t, :], in_=rv[:])
+            store("rv", v_view, t)
 
         def scale_k(wk, rstd_k):
             zk = work.tile([P, B, DH], F32, name="zk")
@@ -315,31 +332,32 @@ def tile_groupqueryattention_pa_t_kernel(
             return zk
 
         def shift_k_on_gpsimd(t, zk):
-            rk = stage.tile([P, B, DH], F32, name="rk")
+            rk = stage_for("rk", t, B)
             nc.gpsimd.tensor_tensor(
-                out=rk[:], in0=zk[:], in1=shift_k[:, t, :].unsqueeze(1).to_broadcast([P, B, DH]), op=ALU.add
+                out=rk, in0=zk[:], in1=shift_k[:, t, :].unsqueeze(1).to_broadcast([P, B, DH]), op=ALU.add
             )
-            return rk
 
         def finish_k_on_vector(t, wk, rstd_k):
-            rk = stage.tile([P, B, DH], F32, name="rk")
+            rk = stage_for("rk", t, B)
             for b in range(B):
                 nc.vector.scalar_tensor_tensor(
                     out=rk[:, b, :], in0=wk[:, b, :], scalar=rstd_k[:, b : b + 1], in1=shift_k[:, t, :],
                     op0=ALU.mult, op1=ALU.add,
                 )
-            return rk
 
         def finish_q(t, prod, rstd_q, shift_q):
-            rq = stage.tile([P, QB, DH], F32, name="rq")
-            step = QB // 2 if t == T - 1 else QB
+            rq = stage_for("rq", t, QB)
             for i in range(QB):
                 nc.vector.scalar_tensor_tensor(
                     out=rq[:, i, :], in0=prod[:, 0, i, :], scalar=rstd_q[:, i : i + 1],
                     in1=shift_q[:, 0, :], op0=ALU.mult, op1=ALU.add,
                 )
-                if (i + 1) % step == 0:
-                    nc.sync.dma_start(out=q_view[:, i + 1 - step : i + 1, t, :], in_=rq[:, i + 1 - step : i + 1, :])
+                if t == T - 1 and i == QB // 2 - 1:
+                    nc.sync.dma_start(out=q_view[:, 0 : QB // 2, t, :], in_=rq[:, 0 : QB // 2, :])
+            if t == T - 1:
+                nc.sync.dma_start(out=q_view[:, QB // 2 : QB, t, :], in_=rq[:, QB // 2 : QB, :])
+            else:
+                store("rq", q_view, t)
 
         def start_group(t):
             banks = transpose_x(t)
@@ -416,16 +434,16 @@ def tile_groupqueryattention_pa_t_kernel(
                     copy_shifts(n, shift, T)
 
                 if n >= 1:
-                    rk = shift_k_on_gpsimd(n - 1, before[3])
-                    nc.sync.dma_start(out=k_view[:, :, n - 1, :], in_=rk[:])
+                    shift_k_on_gpsimd(n - 1, before[3])
+                    store("rk", k_view, n - 1)
                 if n >= 1 and n + 3 < T:
                     build_table(nc.gpsimd, n + 3, n + 4)
                 add_q(prod, ((nc.gpsimd, 0, QB // 2), (nc.gpsimd, QB // 2, QB)))
             if n >= 1:
                 finish_q(n - 1, before[0], before[1], before[2])
             if n == T - 1:
-                rk = finish_k_on_vector(n, wk, rstd_k)
-                nc.sync.dma_start(out=k_view[:, :, n, :], in_=rk[:])
+                finish_k_on_vector(n, wk, rstd_k)
+                store("rk", k_view, n)
             if n + 1 < T:
                 kt_of[n + 1] = project_kt(mx_of[n + 1])
                 kv_of[n + 1] = project(mx_of[n + 1], "kv", K_COL)

@@ -433,12 +433,12 @@ def tile_groupqueryattention_pa_t_kernel(
                 if n == T - 1:
                     copy_shifts(n, shift, T)
 
+                add_q(prod, ((nc.gpsimd, 0, QB // 2), (nc.gpsimd, QB // 2, QB)))
                 if n >= 1:
                     shift_k_on_gpsimd(n - 1, before[3])
                     store("rk", k_view, n - 1)
                 if n >= 1 and n + 3 < T:
                     build_table(nc.gpsimd, n + 3, n + 4)
-                add_q(prod, ((nc.gpsimd, 0, QB // 2), (nc.gpsimd, QB // 2, QB)))
             if n >= 1:
                 finish_q(n - 1, before[0], before[1], before[2])
             if n == T - 1:

@@ -25,7 +25,9 @@ N_ALL = (H + 2) * DH
 K_COL = H * DH
 V_COL = (H + 1) * DH
 QB = B * H
-CHUNK = 4
+CHUNK = 5
+LEAD = 3
+LAST = 4
 
 FLOPS = 2 * B * S * D * N_ALL
 
@@ -63,7 +65,7 @@ def tile_groupqueryattention_pa_t_kernel(
         xpool = ctx.enter_context(tc.tile_pool(name="xpool", bufs=1))
         quant = ctx.enter_context(tc.tile_pool(name="quant", bufs=2))
         work = ctx.enter_context(tc.tile_pool(name="work", bufs=3))
-        stage = ctx.enter_context(tc.tile_pool(name="stage", bufs=3))
+        stage = ctx.enter_context(tc.tile_pool(name="stage", bufs=6))
         psum = ctx.enter_context(tc.psum_pool(name="psum", bufs=1))
 
         x_tiles = []
@@ -107,7 +109,8 @@ def tile_groupqueryattention_pa_t_kernel(
                     in_=scales[0, 4 * quad : 4 * quad + 4, :].bitcast(I32),
                 )
 
-        load_x(0)
+        for j in range(2):
+            nc.sync.dma_start(out=x_tiles[0][:, 2 * j : 2 * j + 2, :], in_=x_view[:, 2 * j : 2 * j + 2, 0, :])
         load_trig(0, CHUNK)
         load_w(wk_words, wk_scales, K_COL)
         load_w(wq_words, wq_scales, 0)
@@ -203,13 +206,20 @@ def tile_groupqueryattention_pa_t_kernel(
             )
             return kt
 
-        def project(mx, kind, c0):
+        def new_banks(kind):
             banks = []
             for j in range(2):
                 bank = psum.tile([P, 2, 2, DH], F32, tag="%s%d" % (kind, j), name=kind)
-                for i in range(2):
-                    pass_x(bank[:, i, :, :].rearrange("p c d -> p (c d)"), mx, 2 * j + i, c0, c0 + 2 * DH)
                 banks.append(bank)
+            return banks
+
+        def fill_banks(banks, mx, c0):
+            for b in range(B):
+                pass_x(banks[b // 2][:, b % 2, :, :].rearrange("p c d -> p (c d)"), mx, b, c0, c0 + 2 * DH)
+
+        def project(mx, kind, c0):
+            banks = new_banks(kind)
+            fill_banks(banks, mx, c0)
             return banks
 
         shift_swap = const.tile([P, 2, DH], BF16)
@@ -309,15 +319,11 @@ def tile_groupqueryattention_pa_t_kernel(
         staged = {}
 
         def stage_for(name, t, blocks):
-            if t % 2 == 0 or t == T - 1:
-                staged[name] = stage.tile([P, blocks, 2, DH], F32, name=name)
-            return staged[name][:, :, t % 2, :]
+            staged[name] = stage.tile([P, blocks, DH], F32, name=name)
+            return staged[name]
 
         def store(name, view, t):
-            if t >= T - 2:
-                nc.sync.dma_start(out=view[:, :, t, :], in_=staged[name][:, :, t % 2, :])
-            elif t % 2 == 1:
-                nc.sync.dma_start(out=view[:, :, t - 1 : t + 1, :], in_=staged[name][:])
+            nc.sync.dma_start(out=view[:, :, t, :], in_=staged[name][:])
 
         def store_v(t, banks):
             rv = stage_for("rv", t, B)
@@ -334,7 +340,7 @@ def tile_groupqueryattention_pa_t_kernel(
         def shift_k_on_gpsimd(t, zk):
             rk = stage_for("rk", t, B)
             nc.gpsimd.tensor_tensor(
-                out=rk, in0=zk[:], in1=shift_k[:, t, :].unsqueeze(1).to_broadcast([P, B, DH]), op=ALU.add
+                out=rk[:, :, :], in0=zk[:], in1=shift_k[:, t, :].unsqueeze(1).to_broadcast([P, B, DH]), op=ALU.add
             )
 
         def finish_k_on_vector(t, wk, rstd_k):
@@ -345,110 +351,114 @@ def tile_groupqueryattention_pa_t_kernel(
                     op0=ALU.mult, op1=ALU.add,
                 )
 
-        def finish_q(t, prod, rstd_q, shift_q):
-            rq = stage_for("rq", t, QB)
-            for i in range(QB):
+        def finish_q(t, i0, i1, prod, rstd_q, shift_q):
+            rq = stage_for("rq", t, QB) if i0 == 0 else staged["rq"]
+            for i in range(i0, i1):
                 nc.vector.scalar_tensor_tensor(
                     out=rq[:, i, :], in0=prod[:, 0, i, :], scalar=rstd_q[:, i : i + 1],
                     in1=shift_q[:, 0, :], op0=ALU.mult, op1=ALU.add,
                 )
-                if t == T - 1 and i == QB // 2 - 1:
-                    nc.sync.dma_start(out=q_view[:, 0 : QB // 2, t, :], in_=rq[:, 0 : QB // 2, :])
-            if t == T - 1:
-                nc.sync.dma_start(out=q_view[:, QB // 2 : QB, t, :], in_=rq[:, QB // 2 : QB, :])
-            else:
-                store("rq", q_view, t)
+            nc.sync.dma_start(out=q_view[:, i0:i1, t, :], in_=rq[:, i0:i1, :])
 
-        def start_group(t):
-            banks = transpose_x(t)
-            grouped = new_group()
-            for j in range(2):
-                group_x(grouped, banks, j)
-            return grouped
-
-        x_banks = transpose_x(0)
         grouped_of = {0: new_group()}
-        group_x(grouped_of[0], x_banks, 0)
-        group_x(grouped_of[0], x_banks, 1, nc.vector.tensor_copy)
+        xt_of = {0: transpose_x(0)}
+        group_x(grouped_of[0], xt_of[0], 0)
+        group_x(grouped_of[0], xt_of[0], 1, nc.vector.tensor_copy)
         swap_sin(nc.vector, 0, CHUNK)
         mx_of = {0: quantise(grouped_of[0])}
         gt = psum.tile([P, P], F32, tag="shift", name="gt")
         nc.tensor.transpose(gt[:], gain[:, 1, :], ident_f32[:])
         nc.scalar.copy(out=gain_k[:], in_=gt[:, 0:1])
-        tp = psum.tile([P, CHUNK, 2, P], BF16, tag="xt", bufs=2, name="tp")
-        for t in range(CHUNK):
+        tp = psum.tile([P, LEAD, 2, P], BF16, tag="xt", bufs=2, name="tp")
+        for t in range(LEAD):
             transpose_trig(tp[:, t, :, :], t)
-        nc.scalar.copy(out=trig_t[:, 0:CHUNK, :, :], in_=tp[:])
-        build_table(nc.vector, 0, 2)
-        kt_of = {0: project_kt(mx_of[0])}
-        q_of = {0: project(mx_of[0], "q", 0)}
-        kv_of = {0: project(mx_of[0], "kv", K_COL)}
-        build_table(nc.gpsimd, 2, CHUNK)
+        nc.scalar.copy(out=trig_t[:, 0:LEAD, :, :], in_=tp[:])
+        build_table(nc.gpsimd, 0, 1)
+        build_table(nc.gpsimd, 1, CHUNK)
+        kt = project_kt(mx_of[0])
+        q = project(mx_of[0], "q", 0)
+        kv = new_banks("kv")
+        for b in range(B):
+            pass_x(kv[b // 2][:, b % 2, 0, :], mx_of[0], b, K_COL, V_COL)
+        sumsq_k = squares([kv[j][:, i, 0, :] for j in range(2) for i in range(2)], "k")
+        xt_of[1] = transpose_x(1)
+        prod_k = multiply_k(0, kt)
+        wk = add_k(prod_k)
+        for b in range(B):
+            pass_x(kv[b // 2][:, b % 2, 1, :], mx_of[0], b, V_COL, N_ALL)
+        rstd_k = inverse_rms(sumsq_k, B, "k")
+        prod = work.tile([P, 2, QB, DH], F32, name="prod")
+        multiply_q(0, q, prod, 0)
+        multiply_q(0, q, prod, 1)
+        grouped_of[1] = new_group()
+        for j in range(2):
+            group_x(grouped_of[1], xt_of[1], j)
+        mx_of[1] = quantise(grouped_of[1])
+        zk = scale_k(wk, rstd_k)
+        store_v(0, kv)
+        xt_of[2] = transpose_x(2)
         nc.vector.tensor_copy(out=shift_swap[:, :, 0:HALF], in_=par_b[:, 2:4, HALF:DH])
         nc.vector.tensor_copy(out=shift_swap[:, :, HALF:DH], in_=par_b[:, 2:4, 0:HALF])
         for out, mat, vec in ((diag_shift, ident_bf, par_b[:, 2:4, :]), (diag_shift_swap, swap_bf, shift_swap[:])):
             nc.vector.tensor_tensor(
                 out=out[:], in0=mat[:].unsqueeze(1).to_broadcast([P, 2, P]), in1=vec, op=ALU.mult
             )
+        sumsq_q = work.tile([P, QB], F32, name="sumsq_q")
+        grouped_of[2] = new_group()
+        for j in range(2):
+            squares_q(sumsq_q, q, j)
+            group_x(grouped_of[2], xt_of[2], j)
+        rstd_q = inverse_rms(sumsq_q, QB, "q")
+        add_q(prod, ((nc.gpsimd, 0, 4), (nc.gpsimd, 4, 6), (nc.gpsimd, 6, 8)))
+        kt_of = {1: project_kt(mx_of[1])}
+        q_of = {1: project(mx_of[1], "q", 0)}
+        kv_of = {1: project(mx_of[1], "kv", K_COL)}
+        before = (prod, rstd_q, rotate_shifts(0, LEAD), zk)
 
-        before = None
-        xt_of = {1: transpose_x(1)}
-        for n in range(T + 1):
-            if n < T:
-                kt, q, kv = kt_of[n], q_of[n], kv_of[n]
-                prod_k = multiply_k(n, kt)
-                wk = add_k(prod_k)
+        for n in range(1, T):
+            last = n == T - 1
+            kt, q, kv = kt_of[n], q_of[n], kv_of[n]
+            prod_k = multiply_k(n, kt)
+            if last:
+                last_shift = rotate_shifts(n, T)
+            wk = add_k(prod_k)
+            if n + 2 < T:
+                xt_of[n + 2] = transpose_x(n + 2)
+            sumsq_k = squares([kv[j][:, i, 0, :] for j in range(2) for i in range(2)], "k")
+            store_v(n, kv)
+            rstd_k = inverse_rms(sumsq_k, B, "k")
+            copy_shifts(n - 1, before[2], n - 1 + LEAD)
+            if last:
+                copy_shifts(n, last_shift, T)
+            prod = work.tile([P, 2, QB, DH], F32, name="prod")
+            if n == 2:
+                swap_sin(nc.vector, CHUNK, T)
+            multiply_q(n, q, prod, 0)
+            if not last:
+                mx_of[n + 1] = quantise(grouped_of[n + 1])
+                zk = scale_k(wk, rstd_k)
+            multiply_q(n, q, prod, 1)
+
+            sumsq_q = work.tile([P, QB], F32, name="sumsq_q")
+            if n + 2 < T:
+                grouped_of[n + 2] = new_group()
+            for j in range(2):
+                squares_q(sumsq_q, q, j)
                 if n + 2 < T:
-                    xt_of[n + 2] = transpose_x(n + 2)
-                prod = work.tile([P, 2, QB, DH], F32, name="prod")
-                multiply_q(n, q, prod, 0)
-                sumsq_k = squares([kv[j][:, i, 0, :] for j in range(2) for i in range(2)], "k")
-                store_v(n, kv)
-                rstd_k = inverse_rms(sumsq_k, B, "k")
-                if n == 0:
-                    grouped_of[1] = new_group()
-                    for j in range(2):
-                        group_x(grouped_of[1], xt_of[1], j)
-                if n >= 1:
-                    copy_shifts(n - 1, before[2], n - 1 + CHUNK)
-                    if n + 1 < T:
-                        mx_of[n + 1] = quantise(grouped_of[n + 1])
-                if n < T - 1:
-                    zk = scale_k(wk, rstd_k)
-                multiply_q(n, q, prod, 1)
-                if n == 0:
-                    mx_of[1] = quantise(grouped_of[1])
-                    swap_sin(nc.vector, CHUNK, T)
-                if n == T - 1:
-                    shift = rotate_shifts(n, T)
-
-                sumsq_q = work.tile([P, QB], F32, name="sumsq_q")
-                if n + 2 < T:
-                    grouped_of[n + 2] = new_group()
-                for j in range(2):
-                    squares_q(sumsq_q, q, j)
-                    if n + 2 < T:
-                        group_x(grouped_of[n + 2], xt_of[n + 2], j)
-                rstd_q = inverse_rms(sumsq_q, QB, "q")
-                if n == T - 1:
-                    copy_shifts(n, shift, T)
-
-                add_q(prod, ((nc.gpsimd, 0, QB // 2), (nc.gpsimd, QB // 2, QB)))
-                if n >= 1:
-                    shift_k_on_gpsimd(n - 1, before[3])
-                    store("rk", k_view, n - 1)
-                if n >= 1 and n + 3 < T:
-                    build_table(nc.gpsimd, n + 3, n + 4)
-            if n >= 1:
-                finish_q(n - 1, before[0], before[1], before[2])
-            if n == T - 1:
-                finish_k_on_vector(n, wk, rstd_k)
-                store("rk", k_view, n)
-            if n + 1 < T:
+                    group_x(grouped_of[n + 2], xt_of[n + 2], j)
+            rstd_q = inverse_rms(sumsq_q, QB, "q")
+            shift_k_on_gpsimd(n - 1, before[3])
+            store("rk", k_view, n - 1)
+            if n >= 2 and n + 3 < T:
+                build_table(nc.gpsimd, n + 3, n + 4)
+            add_q(prod, ((nc.gpsimd, 0, QB // 2), (nc.gpsimd, QB // 2, QB)))
+            finish_q(n - 1, 0, QB, before[0], before[1], before[2])
+            if not last:
                 kt_of[n + 1] = project_kt(mx_of[n + 1])
                 kv_of[n + 1] = project(mx_of[n + 1], "kv", K_COL)
                 q_of[n + 1] = project(mx_of[n + 1], "q", 0)
-            if n < T:
-                if n < T - 1:
-                    shift = rotate_shifts(n, n + CHUNK)
-                before = (prod, rstd_q, shift, zk)
+                before = (prod, rstd_q, rotate_shifts(n, n + LEAD), zk)
+        finish_k_on_vector(T - 1, wk, rstd_k)
+        store("rk", k_view, T - 1)
+        for i in range(0, QB, LAST):
+            finish_q(T - 1, i, i + LAST, prod, rstd_q, last_shift)

@@ -27,7 +27,7 @@ V_COL = (H + 1) * DH
 QB = B * H
 CHUNK = 5
 LEAD = 3
-LAST = 4
+LAST = 2
 
 FLOPS = 2 * B * S * D * N_ALL
 
@@ -451,7 +451,7 @@ def tile_groupqueryattention_pa_t_kernel(
             store("rk", k_view, n - 1)
             if n >= 2 and n + 3 < T:
                 build_table(nc.gpsimd, n + 3, n + 4)
-            add_q(prod, ((nc.gpsimd, 0, QB // 2), (nc.gpsimd, QB // 2, QB)))
+            add_q(prod, ((nc.gpsimd, 0, QB // 2), (nc.gpsimd, QB // 2, QB)) if last else ((nc.gpsimd, 0, QB),))
             finish_q(n - 1, 0, QB, before[0], before[1], before[2])
             if not last:
                 kt_of[n + 1] = project_kt(mx_of[n + 1])

from contextlib import ExitStack

import concourse.mybir as mybir
from concourse.masks import make_identity

F32 = mybir.dt.float32
BF16 = mybir.dt.bfloat16
I32 = mybir.dt.int32
U8 = mybir.dt.uint8
U32 = mybir.dt.uint32
FP8X4 = mybir.dt.float8_e4m3fn_x4
ALU = mybir.AluOpType
ACT = mybir.ActivationFunctionType

P = 128
B = 4
S = 2048
D = 512
H = 2
DH = 128
HALF = DH // 2
EPS = 1e-6
T = S // P
N_ALL = (H + 2) * DH
K_COL = H * DH
V_COL = (H + 1) * DH
QB = B * H
CHUNK = 5
LEAD = 3
LAST = 2

FLOPS = 2 * B * S * D * N_ALL


def tile_groupqueryattention_pa_t_kernel(
    tc,
    x,
    sin_thetas,
    cos_thetas,
    wq_words,
    wq_scales,
    wk_words,
    wk_scales,
    wv_words,
    wv_scales,
    q_scale,
    q_shift,
    k_scale,
    k_shift,
    out_0,
    out_1,
    out_2,
):
    nc = tc.nc
    x_view = x.rearrange("b (p t) k -> p b t k", t=T)
    cos_view = cos_thetas.rearrange("(p t) d -> p t d", t=T)
    sin_view = sin_thetas.rearrange("(p t) d -> p t d", t=T)
    q_view = out_0.rearrange("b h (p t) d -> p (b h) t d", t=T)
    k_view = out_1.rearrange("b h (p t) d -> p (b h) t d", t=T)
    v_view = out_2.rearrange("b h (p t) d -> p (b h) t d", t=T)

    with ExitStack() as ctx:
        ctx.enter_context(tc.manual_schedule())
        const = ctx.enter_context(tc.tile_pool(name="const", bufs=1))
        xpool = ctx.enter_context(tc.tile_pool(name="xpool", bufs=1))
        quant = ctx.enter_context(tc.tile_pool(name="quant", bufs=2))
        work = ctx.enter_context(tc.tile_pool(name="work", bufs=3))
        stage = ctx.enter_context(tc.tile_pool(name="stage", bufs=6))
        psum = ctx.enter_context(tc.psum_pool(name="psum", bufs=1))

        x_tiles = []
        for t in range(T):
            x_sb = xpool.tile([P, B, D], BF16, name="x%d" % t)
            x_tiles.append(x_sb)

        def load_x(t):
            nc.sync.dma_start(out=x_tiles[t][:], in_=x_view[:, :, t, :])

        trig = const.tile([P, T, 2, DH], BF16)
        sin_sb = const.tile([P, T, DH], BF16)

        def load_trig(t0, t1):
            nc.sync.dma_start(out=trig[:, t0:t1, 0, :], in_=cos_view[:, t0:t1, :])
            nc.sync.dma_start(out=sin_sb[:, t0:t1, :], in_=sin_view[:, t0:t1, :])

        def swap_sin(engine, t0, t1):
            engine.tensor_copy(out=trig[:, t0:t1, 1, 0:HALF], in_=sin_sb[:, t0:t1, HALF:DH])
            engine.tensor_scalar(
                out=trig[:, t0:t1, 1, HALF:DH], in0=sin_sb[:, t0:t1, 0:HALF], scalar1=-1.0, scalar2=None, op0=ALU.mult
            )

        par_b = const.tile([P, 4, DH], BF16)
        for i, vec in enumerate((q_scale, k_scale, q_shift, k_shift)):
            nc.scalar.dma_start(out=par_b[:, i, :], in_=vec.partition_broadcast(P))

        w_codes = const.tile([P, 4 * N_ALL], U8, align_bytes=64)
        w_scales = const.tile([P, N_ALL], U8, align_bytes=64)
        nc.vector.memset(w_scales[:].bitcast(I32), 0)

        def load_w(words, scales, col):
            n = words.shape[2]
            nc.sync.dma_start(
                out=w_codes[:, 4 * col : 4 * (col + n)].bitcast(I32),
                in_=words[0].rearrange("p n t -> p (n t)").bitcast(I32),
            )
            for quad in range(4):
                nc.sync.dma_start(
                    out=w_scales[32 * quad : 32 * quad + 4, col : col + n].bitcast(I32),
                    in_=scales[0, 4 * quad : 4 * quad + 4, :].bitcast(I32),
                )

        for j in range(2):
            nc.sync.dma_start(out=x_tiles[0][:, 2 * j : 2 * j + 2, :], in_=x_view[:, 2 * j : 2 * j + 2, 0, :])
        load_trig(0, CHUNK)
        load_w(wk_words, wk_scales, K_COL)
        load_w(wq_words, wq_scales, 0)
        load_x(1)
        load_w(wv_words, wv_scales, V_COL)
        load_x(2)
        load_trig(CHUNK, T)
        for t in range(3, T):
            load_x(t)

        ident_f32 = const.tile([P, P], F32)
        make_identity(nc, ident_f32[:])
        ident_bf = const.tile([P, P], BF16)
        make_identity(nc, ident_bf[:])
        eps_col = const.tile([P, 1], F32)
        nc.vector.memset(eps_col[:], EPS)
        warm = const.tile([P, 1], F32)
        nc.scalar.activation(out=warm[:], in_=eps_col[:], func=ACT.Abs_reciprocal_sqrt)

        def swap_columns(out, in_):
            nc.gpsimd.tensor_copy(out=out[:, 0:HALF], in_=in_[:, HALF:DH])
            nc.gpsimd.tensor_copy(out=out[:, HALF:DH], in_=in_[:, 0:HALF])

        swap_f32 = const.tile([P, P], F32)
        swap_columns(swap_f32, ident_f32)
        swap_bf = const.tile([P, P], BF16)
        swap_columns(swap_bf, ident_bf)

        gain = const.tile([P, 2, DH], F32)
        nc.vector.tensor_scalar_add(out=gain[:], in0=par_b[:, 0:2, :], scalar1=1.0)

        tab = const.tile([P, T, 2, DH], F32)

        def build_table(engine, t0, t1):
            engine.tensor_tensor(
                out=tab[:, t0:t1, :, :],
                in0=trig[:, t0:t1, :, :],
                in1=gain[:, 0, :].unsqueeze(1).unsqueeze(1).to_broadcast([P, t1 - t0, 2, DH]),
                op=ALU.mult,
            )

        def transpose_x(t):
            banks = []
            for j in range(B // 2):
                xt = psum.tile([P, 2, 2, P], F32, tag="xt", bufs=2, name="xt")
                for i in range(2):
                    x_words = x_tiles[t][:, 2 * j + i, :].bitcast(F32)
                    for u in range(2):
                        nc.tensor.transpose(xt[:, i, u, :], x_words[:, u : D // 2 : 2], ident_f32[:])
                banks.append(xt)
            return banks

        def new_group():
            return quant.tile([P, B, P, 2], F32, align_bytes=64, name="grouped")

        def group_x(grouped, banks, j, copy=nc.scalar.copy):
            copy(
                out=grouped[:, 2 * j : 2 * j + 2, :, :],
                in_=banks[j][:].rearrange("p i u r -> p i r u"),
            )

        def quantise(grouped):
            codes = quant.tile([P, B * P], U32, align_bytes=64, bufs=3, name="codes")
            planes = quant.tile([P, B * P], U8, align_bytes=64, bufs=3, name="planes")
            nc.vector.quantize_mx(
                out=codes[:].bitcast(FP8X4),
                scales=planes[:],
                in_=grouped[:].rearrange("p b r u -> p (b r u)").bitcast(BF16),
            )
            return codes, planes

        def pass_x(out, mx, b, c0, c1):
            nc.tensor.matmul_mx(
                out=out,
                lhsT=mx[0][:, b * P : (b + 1) * P].bitcast(FP8X4),
                lhsT_scale=mx[1][:, b * P : (b + 1) * P],
                rhs=w_codes[:, 4 * c0 : 4 * c1].bitcast(FP8X4),
                rhs_scale=w_scales[:, c0:c1],
                start=True,
                stop=True,
            )

        def project_kt(mx):
            kt = psum.tile([P, B, P], F32, tag="kt", name="kt")
            nc.tensor.matmul_mx(
                out=kt[:].rearrange("p b r -> p (b r)"),
                lhsT=w_codes[:, 4 * K_COL : 4 * V_COL].bitcast(FP8X4),
                lhsT_scale=w_scales[:, K_COL:V_COL],
                rhs=mx[0][:].bitcast(FP8X4),
                rhs_scale=mx[1][:],
                start=True,
                stop=True,
            )
            return kt

        def new_banks(kind):
            banks = []
            for j in range(2):
                bank = psum.tile([P, 2, 2, DH], F32, tag="%s%d" % (kind, j), name=kind)
                banks.append(bank)
            return banks

        def fill_banks(banks, mx, c0):
            for b in range(B):
                pass_x(banks[b // 2][:, b % 2, :, :].rearrange("p c d -> p (c d)"), mx, b, c0, c0 + 2 * DH)

        def project(mx, kind, c0):
            banks = new_banks(kind)
            fill_banks(banks, mx, c0)
            return banks

        shift_swap = const.tile([P, 2, DH], BF16)
        diag_shift = const.tile([P, 2, DH], BF16)
        diag_shift_swap = const.tile([P, 2, DH], BF16)
        trig_t = const.tile([P, T, 2, P], BF16)
        shift_k = const.tile([P, T, DH], F32)
        gain_k = const.tile([P, 1], F32)

        def transpose_trig(out, t):
            for c in range(2):
                nc.tensor.transpose(out[:, c, :], trig[:, t, c, :], ident_bf[:])

        def rotate_shifts(t, ahead):
            tag, bufs = ("shift", 1) if t < T - 1 else ("xt", 2)
            bank = psum.tile([P, 4, DH], F32, tag=tag, bufs=bufs, name="bank")
            both = "p c d -> p (c d)"
            for c, diag in enumerate((diag_shift, diag_shift_swap)):
                nc.tensor.matmul(
                    out=bank[:, 0:2, :].rearrange(both), lhsT=trig_t[:, t, c, :], rhs=diag[:].rearrange(both),
                    start=(c == 0), stop=(c == 1),
                )
            if ahead < T:
                transpose_trig(bank[:, 2, :].bitcast(BF16).rearrange("p (c r) -> p c r", c=2), ahead)
            return bank

        def copy_shifts(t, bank, ahead):
            if ahead < T:
                nc.scalar.copy(
                    out=trig_t[:, ahead, :, :],
                    in_=bank[:, 2, :].bitcast(BF16).rearrange("p (c r) -> p c r", c=2),
                )
            nc.scalar.copy(out=shift_k[:, t, :], in_=bank[:, 1, :])

        def squares(blocks, name):
            sumsq = work.tile([P, len(blocks)], F32, name="sumsq_" + name)
            for i, blk in enumerate(blocks):
                junk = work.tile([P, DH], F32, name="junk")
                nc.scalar.activation(out=junk[:], in_=blk, func=ACT.Square, accum_out=sumsq[:, i : i + 1])
            return sumsq

        def squares_q(sumsq, banks, j):
            for i in range(2):
                for h in range(H):
                    junk = work.tile([P, DH], F32, name="junk")
                    c = 4 * j + 2 * i + h
                    nc.scalar.activation(
                        out=junk[:], in_=banks[j][:, i, h, :], func=ACT.Square, accum_out=sumsq[:, c : c + 1]
                    )

        def inverse_rms(sumsq, n, name):
            rstd = work.tile([P, n], F32, name="rstd_" + name)
            nc.scalar.activation(
                out=rstd[:], in_=sumsq[:], func=ACT.Abs_reciprocal_sqrt, bias=eps_col[:, 0:1], scale=1.0 / DH
            )
            return rstd

        def multiply_k(t, kt):
            prod_k = work.tile([P, 2, B, P], F32, name="prod_k")
            for c in range(2):
                nc.vector.scalar_tensor_tensor(
                    out=prod_k[:, c, :, :],
                    in0=kt[:],
                    scalar=gain_k[:, 0:1],
                    in1=trig_t[:, t, c, :].unsqueeze(1).to_broadcast([P, B, P]),
                    op0=ALU.mult,
                    op1=ALU.mult,
                )
            return prod_k

        def add_k(prod_k):
            wk = psum.tile([P, B, P], F32, tag="kt", name="wk")
            for b in range(B):
                for c, perm in enumerate((ident_f32, swap_f32)):
                    nc.tensor.matmul(
                        out=wk[:, b, :], lhsT=prod_k[:, c, b, :], rhs=perm[:], is_transpose=True,
                        start=(c == 0), stop=(c == 1),
                    )
            return wk

        def multiply_q(t, banks, prod, j):
            nc.vector.tensor_tensor(
                out=prod[:, :, 4 * j : 4 * j + 4, :],
                in0=banks[j][:].rearrange("p i h d -> p (i h) d").unsqueeze(1).to_broadcast([P, 2, 4, DH]),
                in1=tab[:, t, :, :].unsqueeze(2).to_broadcast([P, 2, 4, DH]),
                op=ALU.mult,
            )

        def add_q(prod, pieces):
            halves = "p n (h d) -> p n h d"
            for engine, n0, n1 in pieces:
                engine.tensor_tensor(
                    out=prod[:, 0, n0:n1, :].rearrange(halves, h=2), in0=prod[:, 0, n0:n1, :].rearrange(halves, h=2),
                    in1=prod[:, 1, n0:n1, :].rearrange(halves, h=2)[:, :, ::-1, :], op=ALU.add,
                )

        staged = {}

        def stage_for(name, t, blocks):
            staged[name] = stage.tile([P, blocks, DH], F32, name=name)
            return staged[name]

        def store(name, view, t):
            nc.sync.dma_start(out=view[:, :, t, :], in_=staged[name][:])

        def store_v(t, banks):
            rv = stage_for("rv", t, B)
            for j in range(2):
                nc.scalar.copy(out=rv[:, 2 * j : 2 * j + 2, :], in_=banks[j][:, :, 1, :])
            store("rv", v_view, t)

        def scale_k(wk, rstd_k):
            zk = work.tile([P, B, DH], F32, name="zk")
            for b in range(B):
                nc.scalar.activation(out=zk[:, b, :], in_=wk[:, b, :], func=ACT.Copy, scale=rstd_k[:, b : b + 1])
            return zk

        def shift_k_on_gpsimd(t, zk):
            rk = stage_for("rk", t, B)
            nc.gpsimd.tensor_tensor(
                out=rk[:, :, :], in0=zk[:], in1=shift_k[:, t, :].unsqueeze(1).to_broadcast([P, B, DH]), op=ALU.add
            )

        def finish_k_on_vector(t, wk, rstd_k):
            rk = stage_for("rk", t, B)
            for b in range(B):
                nc.vector.scalar_tensor_tensor(
                    out=rk[:, b, :], in0=wk[:, b, :], scalar=rstd_k[:, b : b + 1], in1=shift_k[:, t, :],
                    op0=ALU.mult, op1=ALU.add,
                )

        def finish_q(t, i0, i1, prod, rstd_q, shift_q):
            rq = stage_for("rq", t, QB) if i0 == 0 else staged["rq"]
            for i in range(i0, i1):
                nc.vector.scalar_tensor_tensor(
                    out=rq[:, i, :], in0=prod[:, 0, i, :], scalar=rstd_q[:, i : i + 1],
                    in1=shift_q[:, 0, :], op0=ALU.mult, op1=ALU.add,
                )
            nc.sync.dma_start(out=q_view[:, i0:i1, t, :], in_=rq[:, i0:i1, :])

        grouped_of = {0: new_group()}
        xt_of = {0: transpose_x(0)}
        group_x(grouped_of[0], xt_of[0], 0)
        group_x(grouped_of[0], xt_of[0], 1, nc.vector.tensor_copy)
        swap_sin(nc.vector, 0, CHUNK)
        mx_of = {0: quantise(grouped_of[0])}
        gt = psum.tile([P, P], F32, tag="shift", name="gt")
        nc.tensor.transpose(gt[:], gain[:, 1, :], ident_f32[:])
        nc.scalar.copy(out=gain_k[:], in_=gt[:, 0:1])
        tp = psum.tile([P, LEAD, 2, P], BF16, tag="xt", bufs=2, name="tp")
        for t in range(LEAD):
            transpose_trig(tp[:, t, :, :], t)
        nc.scalar.copy(out=trig_t[:, 0:LEAD, :, :], in_=tp[:])
        build_table(nc.gpsimd, 0, 1)
        build_table(nc.gpsimd, 1, CHUNK)
        kt = project_kt(mx_of[0])
        q = project(mx_of[0], "q", 0)
        kv = new_banks("kv")
        for b in range(B):
            pass_x(kv[b // 2][:, b % 2, 0, :], mx_of[0], b, K_COL, V_COL)
        sumsq_k = squares([kv[j][:, i, 0, :] for j in range(2) for i in range(2)], "k")
        xt_of[1] = transpose_x(1)
        prod_k = multiply_k(0, kt)
        wk = add_k(prod_k)
        for b in range(B):
            pass_x(kv[b // 2][:, b % 2, 1, :], mx_of[0], b, V_COL, N_ALL)
        rstd_k = inverse_rms(sumsq_k, B, "k")
        prod = work.tile([P, 2, QB, DH], F32, name="prod")
        multiply_q(0, q, prod, 0)
        multiply_q(0, q, prod, 1)
        grouped_of[1] = new_group()
        for j in range(2):
            group_x(grouped_of[1], xt_of[1], j)
        mx_of[1] = quantise(grouped_of[1])
        zk = scale_k(wk, rstd_k)
        store_v(0, kv)
        xt_of[2] = transpose_x(2)
        nc.vector.tensor_copy(out=shift_swap[:, :, 0:HALF], in_=par_b[:, 2:4, HALF:DH])
        nc.vector.tensor_copy(out=shift_swap[:, :, HALF:DH], in_=par_b[:, 2:4, 0:HALF])
        for out, mat, vec in ((diag_shift, ident_bf, par_b[:, 2:4, :]), (diag_shift_swap, swap_bf, shift_swap[:])):
            nc.vector.tensor_tensor(
                out=out[:], in0=mat[:].unsqueeze(1).to_broadcast([P, 2, P]), in1=vec, op=ALU.mult
            )
        sumsq_q = work.tile([P, QB], F32, name="sumsq_q")
        grouped_of[2] = new_group()
        for j in range(2):
            squares_q(sumsq_q, q, j)
            group_x(grouped_of[2], xt_of[2], j)
        rstd_q = inverse_rms(sumsq_q, QB, "q")
        add_q(prod, ((nc.gpsimd, 0, 4), (nc.gpsimd, 4, 6), (nc.gpsimd, 6, 8)))
        kt_of = {1: project_kt(mx_of[1])}
        q_of = {1: project(mx_of[1], "q", 0)}
        kv_of = {1: project(mx_of[1], "kv", K_COL)}
        before = (prod, rstd_q, rotate_shifts(0, LEAD), zk)

        for n in range(1, T):
            last = n == T - 1
            kt, q, kv = kt_of[n], q_of[n], kv_of[n]
            prod_k = multiply_k(n, kt)
            if last:
                last_shift = rotate_shifts(n, T)
            wk = add_k(prod_k)
            if n + 2 < T:
                xt_of[n + 2] = transpose_x(n + 2)
            sumsq_k = squares([kv[j][:, i, 0, :] for j in range(2) for i in range(2)], "k")
            store_v(n, kv)
            rstd_k = inverse_rms(sumsq_k, B, "k")
            copy_shifts(n - 1, before[2], n - 1 + LEAD)
            if last:
                copy_shifts(n, last_shift, T)
            prod = work.tile([P, 2, QB, DH], F32, name="prod")
            if n == 2:
                swap_sin(nc.vector, CHUNK, T)
            multiply_q(n, q, prod, 0)
            if not last:
                mx_of[n + 1] = quantise(grouped_of[n + 1])
                zk = scale_k(wk, rstd_k)
            multiply_q(n, q, prod, 1)

            sumsq_q = work.tile([P, QB], F32, name="sumsq_q")
            if n + 2 < T:
                grouped_of[n + 2] = new_group()
            for j in range(2):
                squares_q(sumsq_q, q, j)
                if n + 2 < T:
                    group_x(grouped_of[n + 2], xt_of[n + 2], j)
            rstd_q = inverse_rms(sumsq_q, QB, "q")
            shift_k_on_gpsimd(n - 1, before[3])
            store("rk", k_view, n - 1)
            if n >= 2 and n + 3 < T:
                build_table(nc.gpsimd, n + 3, n + 4)
            add_q(prod, ((nc.gpsimd, 0, QB // 2), (nc.gpsimd, QB // 2, QB)) if last else ((nc.gpsimd, 0, QB),))
            finish_q(n - 1, 0, QB, before[0], before[1], before[2])
            if not last:
                kt_of[n + 1] = project_kt(mx_of[n + 1])
                kv_of[n + 1] = project(mx_of[n + 1], "kv", K_COL)
                q_of[n + 1] = project(mx_of[n + 1], "q", 0)
                before = (prod, rstd_q, rotate_shifts(n, n + LEAD), zk)
        finish_k_on_vector(T - 1, wk, rstd_k)
        store("rk", k_view, T - 1)
        for i in range(0, QB, LAST):
            finish_q(T - 1, i, i + LAST, prod, rstd_q, last_shift)
